import numpy as np
import ml_dtypes


def mxq(x, axis, fmt="e4m3"):
    dtype, down = {"e4m3": (ml_dtypes.float8_e4m3fn, 7), "e5m2": (ml_dtypes.float8_e5m2, 14)}[fmt]
    v = np.moveaxis(np.asarray(x, np.float32).astype(ml_dtypes.bfloat16).astype(np.float64), axis, -1)
    blocks = v.reshape(v.shape[:-1] + (-1, 32))
    amax = np.abs(blocks).max(-1, keepdims=True)
    byte = np.maximum(np.where(amax > 0, np.frexp(amax)[1] - 1 + 127, 0) - down, 1)
    scale = np.exp2(byte - 127.0)
    codes = (blocks / scale).astype(np.float32).astype(dtype).astype(np.float64)
    return np.moveaxis((codes * scale).reshape(v.shape), -1, axis)


WIDE = False


def mx_kscale(k):
    if not WIDE:
        return np.ones(k)
    levels = np.array([10, -10, 5, -5, 0])
    a = np.random.permutation(np.resize(levels, k // 512 * 4)).reshape(k // 512, 4)
    idx = np.arange(k)
    return np.exp2(a[idx // 512, idx % 128 // 32])


BF16 = ml_dtypes.bfloat16


def bf(x):
    return np.asarray(x, np.float32).astype(BF16)


def f64(x):
    return np.asarray(x).astype(np.float64)


B, D, H, F, C, R = 8192, 512, 1024, 1024, 128, 32
P_FACTOR = 3.0
RHO = 0.75
P_LABEL = 0.1


def unit_rows(x):
    return x / np.sqrt((x ** 2).sum(-1, keepdims=True))


def setup_inputs():
    s = mx_kscale(F)
    u = np.exp2(np.round(np.log2(mx_kscale(D)) / P_FACTOR))
    basis = np.random.standard_normal((R, F))
    off = np.random.standard_normal(F) * 0.1
    f = np.random.standard_normal((B, R)) @ basis * np.sqrt(RHO / R) + np.sqrt(1.0 - RHO) * np.random.standard_normal((B, F)) + off
    e = np.random.standard_normal((D, R)) @ basis * np.sqrt(RHO / R) + np.sqrt(1.0 - RHO) * np.random.standard_normal((D, F)) + off
    return {"f_n": bf(unit_rows(f) * s),
            "ex_n": bf(unit_rows(e) / s * u[:, None]),
            "ex_classes": bf((np.random.uniform(size=(D, C)) < P_LABEL) / (u * u * u)[:, None]),
            "class_reps": bf(np.eye(C) + np.random.standard_normal((C, C)) / np.sqrt(C))}


def reference(f_n, ex_n, ex_classes, class_reps):
    s = mxq(f64(f_n), 1, "e4m3") @ mxq(f64(ex_n), 1, "e4m3").T
    a = np.sign(s) * np.abs(s) ** P_FACTOR
    ex_class_reps = f64(ex_classes) @ f64(class_reps)
    echo = mxq(a, 1, "e4m3") @ mxq(ex_class_reps, 0, "e4m3")
    d2 = np.stack([((echo - r) ** 2).sum(-1) for r in f64(class_reps)], axis=1)
    return -np.sqrt(d2)

@@ -1,0 +1,346 @@
+from contextlib import ExitStack
+
+import concourse.bass as bass
+import concourse.mybir as mybir
+import concourse.tile as tile
+from concourse.masks import make_identity
+
+F32 = mybir.dt.float32
+BF16 = mybir.dt.bfloat16
+U32 = mybir.dt.uint32
+U8 = mybir.dt.uint8
+FP8X4 = mybir.dt.float8_e4m3fn_x4
+ACT = mybir.ActivationFunctionType
+ALU = mybir.AluOpType
+
+P = 128
+B, D, F, C = 8192, 512, 1024, 128
+FLOPS = 2 * B * D * F + 2 * B * D * C + 2 * D * C * C + 3 * B * C * C
+
+MANUAL = False
+N_TILES = B // P
+N_MACRO = N_TILES // 4
+N_HALF = N_TILES // 2
+
+
+def tile_minerva_detex_pb_t_kernel(tc, f_n, ex_n, ex_classes, class_reps, out):
+    nc = tc.nc
+    with ExitStack() as ctx:
+        const = ctx.enter_context(tc.tile_pool(name="const", bufs=1))
+        fpool = ctx.enter_context(tc.tile_pool(name="fpool", bufs=N_MACRO))
+        fgp = ctx.enter_context(tc.tile_pool(name="fgp", bufs=4))
+        fcp = ctx.enter_context(tc.tile_pool(name="fcp", bufs=6))
+        s2p = ctx.enter_context(tc.tile_pool(name="s2p", bufs=3))
+        agp = ctx.enter_context(tc.tile_pool(name="agp", bufs=4))
+        acp = ctx.enter_context(tc.tile_pool(name="acp", bufs=3))
+        e3p = ctx.enter_context(tc.tile_pool(name="e3p", bufs=3))
+        ps_xt = ctx.enter_context(tc.psum_pool(name="ps_xt", bufs=2))
+        ps_st = ctx.enter_context(tc.psum_pool(name="ps_st", bufs=4))
+        ps_s3 = ctx.enter_context(tc.psum_pool(name="ps_s3", bufs=2))
+        if MANUAL:
+            ctx.enter_context(tc.manual_schedule())
+
+        ex_sb = const.tile([P, 4 * F], BF16, name="ex_sb")
+        nc.sync.dma_start(
+            out=ex_sb[:].rearrange("p (t k) -> p t k", t=4),
+            in_=ex_n.rearrange("(p t) k -> p t k", t=4),
+        )
+        f_tiles = []
+        for m in range(N_MACRO):
+            f_sb = fpool.tile([P, 4 * F], BF16, name="f_sb", tag="f_sb")
+            f_tiles.append(f_sb)
+
+        def load_f(m):
+            nc.sync.dma_start(
+                out=f_tiles[m][:].rearrange("p (j k) -> p j k", j=4),
+                in_=f_n[512 * m : 512 * (m + 1), :].rearrange("(p j) k -> p j k", j=4),
+            )
+
+        load_f(0)
+        exc_sb = const.tile([P, 4 * C], BF16, name="exc_sb")
+        nc.sync.dma_start(
+            out=exc_sb[:].rearrange("p (t j) -> p t j", t=4),
+            in_=ex_classes.rearrange("(p t) j -> p t j", t=4),
+        )
+        r_sb = const.tile([P, C], BF16, name="r_sb")
+        nc.sync.dma_start(out=r_sb[:], in_=class_reps)
+        for m in range(1, N_MACRO):
+            load_f(m)
+
+        ident = const.tile([P, P], F32, name="ident")
+        make_identity(nc, ident[:])
+        ident_b = const.tile([P, P], BF16, name="ident_b")
+        make_identity(nc, ident_b[:])
+        warm = const.tile([P, 1], F32, name="warm")
+        nc.vector.memset(warm[:], 1.0)
+        nc.scalar.activation(out=warm[:], in_=warm[:], func=ACT.Sqrt)
+        ones_f = const.tile([P, P], F32, name="ones_f")
+        nc.vector.memset(ones_f[:], 1.0)
+        sel = const.tile([P, P], BF16, name="sel")
+        nc.vector.memset(sel[:], 1.0 / 32.0)
+        nc.vector.memset(sel[96:128, :], 0.0)
+
+        ex_c = const.tile([P, 4 * 256], U32, name="ex_c", align_bytes=64)
+        ex_s = const.tile([P, 4 * 256], U8, name="ex_s", align_bytes=64)
+        exw = ex_sb[:].bitcast(F32)
+        exgs = []
+        for t in range(4):
+            xe = ps_st.tile([P, 2, 2, P], F32, name="xe", tag="st")
+            for g in range(2):
+                for u in range(2):
+                    c0 = 512 * t + 256 * g + 128 * u
+                    nc.tensor.transpose(xe[:, g, u, :], exw[:, c0 : c0 + P], ident[:])
+            exg = const.tile([P, 1024], BF16, name="exg%d" % t, align_bytes=64)
+            dst = exg[:].bitcast(F32).rearrange("p (g b u) -> p g b u", g=2, u=2)
+            src = xe[:].rearrange("p g u b -> p g b u")
+            if t % 2 == 0:
+                nc.vector.tensor_copy(out=dst, in_=src)
+            else:
+                nc.scalar.copy(out=dst, in_=src)
+            exgs.append(exg)
+        for t in range(4):
+            nc.vector.quantize_mx(
+                out=ex_c[:, 256 * t : 256 * (t + 1)].bitcast(FP8X4),
+                scales=ex_s[:, 256 * t : 256 * (t + 1)],
+                in_=exgs[t][:],
+            )
+
+        xts = {}
+        fgs = {}
+        fcs = {}
+        sts = {}
+        s2s = {}
+        ags = {}
+        acs = {}
+        c3 = {}
+
+        def do_T(i):
+            m, j = divmod(i, 4)
+            xt = ps_xt.tile([P, 2, 2, P], F32, name="xt", tag="xt")
+            fw = f_tiles[m][:].bitcast(F32)
+            for g in range(2):
+                for u in range(2):
+                    c0 = 512 * j + 256 * g + 128 * u
+                    nc.tensor.transpose(xt[:, g, u, :], fw[:, c0 : c0 + P], ident[:])
+            xts[i] = xt
+
+        def do_E(i, on_vector):
+            fg = fgp.tile([P, 1024], BF16, name="fg", tag="fg", align_bytes=64)
+            dst = fg[:].bitcast(F32).rearrange("p (g b u) -> p g b u", g=2, u=2)
+            src = xts[i][:].rearrange("p g u b -> p g b u")
+            if on_vector:
+                nc.vector.tensor_copy(out=dst, in_=src)
+            else:
+                nc.scalar.copy(out=dst, in_=src)
+            fgs[i] = fg
+
+        def do_Q(i):
+            fc = fcp.tile([P, 256], U32, name="fc", tag="fc", align_bytes=64)
+            fs = fcp.tile([P, 256], U8, name="fs", tag="fs", align_bytes=64)
+            nc.vector.quantize_mx(out=fc[:].bitcast(FP8X4), scales=fs[:], in_=fgs[i][:])
+            fcs[i] = (fc, fs)
+
+        def do_M(i):
+            fc, fs = fcs[i]
+            st = ps_st.tile([P, 4, P], F32, name="st", tag="st")
+            for t in range(4):
+                for g in range(2):
+                    w0 = (2 * t + g) * P
+                    nc.tensor.matmul_mx(
+                        out=st[:, t, :],
+                        lhsT=ex_c[:, w0 : w0 + P].bitcast(FP8X4),
+                        lhsT_scale=ex_s[:, w0 : w0 + P],
+                        rhs=fc[:, g * P : (g + 1) * P].bitcast(FP8X4),
+                        rhs_scale=fs[:, g * P : (g + 1) * P],
+                        start=(g == 0),
+                        stop=(g == 1),
+                    )
+            sts[i] = st
+
+        def do_S(i):
+            s2 = s2p.tile([P, 512], F32, name="s2", tag="s2")
+            nc.scalar.activation(
+                out=s2[:].rearrange("p (b t) -> p b t", t=4),
+                in_=sts[i][:].rearrange("p t b -> p b t"),
+                func=ACT.Square,
+            )
+            s2s[i] = s2
+
+        def do_V(i):
+            ag = agp.tile([P, 512], BF16, name="ag", tag="ag", align_bytes=64)
+            nc.vector.tensor_tensor(
+                out=ag[:].rearrange("p (b t) -> p b t", t=4),
+                in0=sts[i][:].rearrange("p t b -> p b t"),
+                in1=s2s[i][:].rearrange("p (b t) -> p b t", t=4),
+                op=ALU.mult,
+            )
+            ags[i] = ag
+
+        def do_QA(i):
+            m, j = divmod(i, 4)
+            if j == 0:
+                ac = acp.tile([P, 512], U32, name="ac", tag="ac", align_bytes=64)
+                asc = acp.tile([P, 512], U8, name="asc", tag="asc", align_bytes=64)
+                acs[m] = (ac, asc)
+            ac, asc = acs[m]
+            nc.vector.quantize_mx(
+                out=ac[:, j * P : (j + 1) * P].bitcast(FP8X4),
+                scales=asc[:, j * P : (j + 1) * P],
+                in_=ags[i][:],
+            )
+
+        xc_ps = ps_s3.tile([P, 4, P], BF16, name="xc_ps", tag="s3")
+        for t in range(4):
+            nc.tensor.transpose(xc_ps[:, t, :], exc_sb[:, t * P : (t + 1) * P], ident_b[:])
+        excT = const.tile([P, 4, P], BF16, name="excT")
+        nc.vector.tensor_copy(out=excT[:], in_=xc_ps[:])
+        ec_ps = ps_s3.tile([P, 4, P], F32, name="ec_ps", tag="s3")
+        for t in range(4):
+            nc.tensor.matmul(out=ec_ps[:, t, :], lhsT=excT[:, t, :], rhs=r_sb[:], start=True, stop=True)
+        ecg = const.tile([P, 512], BF16, name="ecg", align_bytes=64)
+        nc.vector.tensor_copy(
+            out=ecg[:].rearrange("p (c t) -> p c t", t=4), in_=ec_ps[:].rearrange("p t c -> p c t")
+        )
+        rt_ps = ps_s3.tile([P, P], BF16, name="rt_ps", tag="s3")
+        nc.tensor.transpose(rt_ps[:], r_sb[:], ident_b[:])
+        rTf = const.tile([P, P], F32, name="rTf")
+        nc.vector.tensor_copy(out=rTf[:], in_=rt_ps[:])
+        ecr_c = const.tile([P, P], U32, name="ecr_c", align_bytes=64)
+        ecr_s = const.tile([P, P], U8, name="ecr_s", align_bytes=64)
+        nc.vector.quantize_mx(out=ecr_c[:].bitcast(FP8X4), scales=ecr_s[:], in_=ecg[:])
+        rTm2 = const.tile([P, P], F32, name="rTm2")
+        nc.vector.tensor_scalar(out=rTm2[:], in0=rTf[:], scalar1=-2.0, scalar2=None, op0=ALU.mult)
+        r2T = const.tile([P, P], F32, name="r2T")
+        nc.vector.tensor_tensor(out=r2T[:], in0=rTf[:], in1=rTf[:], op=ALU.mult)
+        rr_ps = ps_s3.tile([P, P], F32, name="rr_ps", tag="s3")
+        nc.tensor.matmul(out=rr_ps[:], lhsT=ones_f[:], rhs=r2T[:], start=True, stop=True)
+        rrf = const.tile([P, P], F32, name="rrf")
+        nc.vector.tensor_copy(out=rrf[:], in_=rr_ps[:])
+        rr_h = const.tile([P, P], BF16, name="rr_h")
+        nc.vector.tensor_copy(out=rr_h[:], in_=rrf[:])
+        rr_d = const.tile([P, P], F32, name="rr_d")
+        nc.vector.tensor_tensor(out=rr_d[:], in0=rrf[:], in1=rr_h[:], op=ALU.subtract)
+        rr_m = const.tile([P, P], BF16, name="rr_m")
+        nc.vector.tensor_copy(out=rr_m[:], in_=rr_d[:])
+        rr_w = const.tile([P, P], BF16, name="rr_w")
+        nc.vector.memset(rr_w[:], 0.0)
+        nc.vector.tensor_copy(out=rr_w[0:32, :], in_=rr_h[0:32, :])
+        nc.vector.tensor_copy(out=rr_w[32:64, :], in_=rr_m[32:64, :])
+        nc.vector.tensor_tensor(out=rr_w[64:96, :], in0=rr_d[64:96, :], in1=rr_m[64:96, :], op=ALU.subtract)
+
+        def do_C_pe(m):
+            ac, asc = acs[m]
+            eT = ps_s3.tile([P, 512], F32, name="eT", tag="s3")
+            nc.tensor.matmul_mx(
+                out=eT[:],
+                lhsT=ecr_c[:].bitcast(FP8X4),
+                lhsT_scale=ecr_s[:],
+                rhs=ac[:].bitcast(FP8X4),
+                rhs_scale=asc[:],
+                start=True,
+                stop=True,
+            )
+            eb = ps_s3.tile([P, 4, P], F32, name="eb", tag="s3")
+            for j in range(4):
+                nc.tensor.matmul_mx(
+                    out=eb[:, j, :],
+                    lhsT=ac[:, j * P : (j + 1) * P].bitcast(FP8X4),
+                    lhsT_scale=asc[:, j * P : (j + 1) * P],
+                    rhs=ecr_c[:].bitcast(FP8X4),
+                    rhs_scale=ecr_s[:],
+                    start=True,
+                    stop=True,
+                )
+            c3[m] = {"eT": eT, "eb": eb}
+
+        def do_C_v(m):
+            eTs = e3p.tile([P, 512], F32, name="eTs", tag="eTs")
+            nc.vector.tensor_copy(out=eTs[:], in_=c3[m]["eT"][:])
+            c3[m]["eTs"] = eTs
+
+        def do_C_s(m):
+            ee = e3p.tile([P, 4], F32, name="ee", tag="ee")
+            for j in range(4):
+                junk = e3p.tile([P, P], BF16, name="junk", tag="junk")
+                nc.scalar.activation(
+                    out=junk[:], in_=c3[m]["eb"][:, j, :], func=ACT.Square, accum_out=ee[:, j : j + 1]
+                )
+            c3[m]["ee"] = ee
+
+        def do_D_pe(m):
+            db = ps_s3.tile([P, 4, P], F32, name="db", tag="s3")
+            eTs = c3[m]["eTs"]
+            for j in range(4):
+                nc.tensor.matmul(out=db[:, j, :], lhsT=sel[:], rhs=rr_w[:], start=True, stop=False)
+                nc.tensor.matmul(
+                    out=db[:, j, :], lhsT=eTs[:, j * P : (j + 1) * P], rhs=rTm2[:], start=False, stop=True
+                )
+            c3[m]["db"] = db
+
+        def do_D_s(m):
+            sq = e3p.tile([P, 512], F32, name="sq", tag="sq")
+            for j in range(4):
+                nc.scalar.activation(
+                    out=sq[:, j * P : (j + 1) * P],
+                    in_=c3[m]["db"][:, j, :],
+                    func=ACT.Sqrt,
+                    bias=c3[m]["ee"][:, j : j + 1],
+                    scale=1.0,
+                )
+            c3[m]["sq"] = sq
+
+        def do_D_v(m):
+            o = e3p.tile([P, 512], F32, name="o", tag="o")
+            nc.vector.tensor_scalar(
+                out=o[:], in0=c3[m]["sq"][:], scalar1=-1.0, scalar2=0.0, op0=ALU.mult, op1=ALU.min
+            )
+            nc.sync.dma_start(
+                out=out[512 * m : 512 * (m + 1), :].rearrange("(p j) k -> p j k", j=4),
+                in_=o[:].rearrange("p (j k) -> p j k", j=4),
+            )
+
+        do_T(0)
+        do_T(1)
+        do_E(0, False)
+        do_E(1, True)
+        do_Q(0)
+        do_Q(1)
+        for h in range(N_HALF + 3):
+            i0, i1 = 2 * h, 2 * h + 1
+            n0, n1 = i0 + 2, i1 + 2
+            nxt = n1 < N_TILES
+            cur = i1 < N_TILES
+            mc = (h - 2) // 2 if (h % 2 == 0 and 2 <= h <= N_HALF) else -1
+            md = (h - 3) // 2 if (h % 2 == 1 and 3 <= h) else -1
+            mn = (h - 4) // 2 if (h % 2 == 0 and 4 <= h) else -1
+            if nxt:
+                do_T(n0)
+                do_T(n1)
+                do_E(n0, False)
+                do_E(n1, h % 2 == 1)
+            if mc >= 0:
+                do_C_pe(mc)
+            if cur:
+                do_M(i0)
+                do_M(i1)
+            if mc >= 0:
+                do_C_v(mc)
+                do_C_s(mc)
+            if cur:
+                do_S(i0)
+                do_V(i0)
+            if mn >= 0:
+                do_D_v(mn)
+            if nxt:
+                do_Q(n0)
+            if cur:
+                do_S(i1)
+                do_V(i1)
+                do_QA(i0)
+            if nxt:
+                do_Q(n1)
+            if cur:
+                do_QA(i1)
+            if md >= 0:
+                do_D_pe(md)
+                do_D_s(md)

@@ -17,7 +17,7 @@ P = 128
 B, D, F, C = 8192, 512, 1024, 128
 FLOPS = 2 * B * D * F + 2 * B * D * C + 2 * D * C * C + 3 * B * C * C
 
-MANUAL = False
+MANUAL = True
 N_TILES = B // P
 N_MACRO = N_TILES // 4
 N_HALF = N_TILES // 2
@@ -28,23 +28,24 @@ def tile_minerva_detex_pb_t_kernel(tc, f_n, ex_n, ex_classes, class_reps, out):
     with ExitStack() as ctx:
         const = ctx.enter_context(tc.tile_pool(name="const", bufs=1))
         fpool = ctx.enter_context(tc.tile_pool(name="fpool", bufs=N_MACRO))
-        fgp = ctx.enter_context(tc.tile_pool(name="fgp", bufs=4))
-        fcp = ctx.enter_context(tc.tile_pool(name="fcp", bufs=6))
+        fgp = ctx.enter_context(tc.tile_pool(name="fgp", bufs=5))
+        fcp = ctx.enter_context(tc.tile_pool(name="fcp", bufs=8))
         s2p = ctx.enter_context(tc.tile_pool(name="s2p", bufs=3))
         agp = ctx.enter_context(tc.tile_pool(name="agp", bufs=4))
         acp = ctx.enter_context(tc.tile_pool(name="acp", bufs=3))
         e3p = ctx.enter_context(tc.tile_pool(name="e3p", bufs=3))
-        ps_xt = ctx.enter_context(tc.psum_pool(name="ps_xt", bufs=2))
-        ps_st = ctx.enter_context(tc.psum_pool(name="ps_st", bufs=4))
+        ps_xt = ctx.enter_context(tc.psum_pool(name="ps_xt", bufs=4))
+        ps_st = ctx.enter_context(tc.psum_pool(name="ps_st", bufs=2))
         ps_s3 = ctx.enter_context(tc.psum_pool(name="ps_s3", bufs=2))
         if MANUAL:
             ctx.enter_context(tc.manual_schedule())
 
-        ex_sb = const.tile([P, 4 * F], BF16, name="ex_sb")
-        nc.sync.dma_start(
-            out=ex_sb[:].rearrange("p (t k) -> p t k", t=4),
-            in_=ex_n.rearrange("(p t) k -> p t k", t=4),
-        )
+        ex_rows = ex_n.rearrange("(p t) k -> p t k", t=4)
+        ex_sbs = []
+        for t in range(4):
+            ex_sb = const.tile([P, F], BF16, name="ex_sb%d" % t)
+            nc.sync.dma_start(out=ex_sb[:], in_=ex_rows[:, t, :])
+            ex_sbs.append(ex_sb)
         f_tiles = []
         for m in range(N_MACRO):
             f_sb = fpool.tile([P, 4 * F], BF16, name="f_sb", tag="f_sb")
@@ -82,13 +83,13 @@ def tile_minerva_detex_pb_t_kernel(tc, f_n, ex_n, ex_classes, class_reps, out):
 
         ex_c = const.tile([P, 4 * 256], U32, name="ex_c", align_bytes=64)
         ex_s = const.tile([P, 4 * 256], U8, name="ex_s", align_bytes=64)
-        exw = ex_sb[:].bitcast(F32)
         exgs = []
         for t in range(4):
-            xe = ps_st.tile([P, 2, 2, P], F32, name="xe", tag="st")
+            xe = ps_xt.tile([P, 2, 2, P], F32, name="xe", tag="xt")
+            exw = ex_sbs[t][:].bitcast(F32)
             for g in range(2):
                 for u in range(2):
-                    c0 = 512 * t + 256 * g + 128 * u
+                    c0 = 256 * g + 128 * u
                     nc.tensor.transpose(xe[:, g, u, :], exw[:, c0 : c0 + P], ident[:])
             exg = const.tile([P, 1024], BF16, name="exg%d" % t, align_bytes=64)
             dst = exg[:].bitcast(F32).rearrange("p (g b u) -> p g b u", g=2, u=2)
@@ -189,44 +190,50 @@ def tile_minerva_detex_pb_t_kernel(tc, f_n, ex_n, ex_classes, class_reps, out):
                 in_=ags[i][:],
             )
 
-        xc_ps = ps_s3.tile([P, 4, P], BF16, name="xc_ps", tag="s3")
-        for t in range(4):
-            nc.tensor.transpose(xc_ps[:, t, :], exc_sb[:, t * P : (t + 1) * P], ident_b[:])
         excT = const.tile([P, 4, P], BF16, name="excT")
-        nc.vector.tensor_copy(out=excT[:], in_=xc_ps[:])
-        ec_ps = ps_s3.tile([P, 4, P], F32, name="ec_ps", tag="s3")
-        for t in range(4):
-            nc.tensor.matmul(out=ec_ps[:, t, :], lhsT=excT[:, t, :], rhs=r_sb[:], start=True, stop=True)
-        ecg = const.tile([P, 512], BF16, name="ecg", align_bytes=64)
-        nc.vector.tensor_copy(
-            out=ecg[:].rearrange("p (c t) -> p c t", t=4), in_=ec_ps[:].rearrange("p t c -> p c t")
-        )
-        rt_ps = ps_s3.tile([P, P], BF16, name="rt_ps", tag="s3")
-        nc.tensor.transpose(rt_ps[:], r_sb[:], ident_b[:])
         rTf = const.tile([P, P], F32, name="rTf")
-        nc.vector.tensor_copy(out=rTf[:], in_=rt_ps[:])
+        ecg = const.tile([P, 512], BF16, name="ecg", align_bytes=64)
         ecr_c = const.tile([P, P], U32, name="ecr_c", align_bytes=64)
         ecr_s = const.tile([P, P], U8, name="ecr_s", align_bytes=64)
-        nc.vector.quantize_mx(out=ecr_c[:].bitcast(FP8X4), scales=ecr_s[:], in_=ecg[:])
         rTm2 = const.tile([P, P], F32, name="rTm2")
-        nc.vector.tensor_scalar(out=rTm2[:], in0=rTf[:], scalar1=-2.0, scalar2=None, op0=ALU.mult)
         r2T = const.tile([P, P], F32, name="r2T")
-        nc.vector.tensor_tensor(out=r2T[:], in0=rTf[:], in1=rTf[:], op=ALU.mult)
-        rr_ps = ps_s3.tile([P, P], F32, name="rr_ps", tag="s3")
-        nc.tensor.matmul(out=rr_ps[:], lhsT=ones_f[:], rhs=r2T[:], start=True, stop=True)
-        rrf = const.tile([P, P], F32, name="rrf")
-        nc.vector.tensor_copy(out=rrf[:], in_=rr_ps[:])
-        rr_h = const.tile([P, P], BF16, name="rr_h")
-        nc.vector.tensor_copy(out=rr_h[:], in_=rrf[:])
-        rr_d = const.tile([P, P], F32, name="rr_d")
-        nc.vector.tensor_tensor(out=rr_d[:], in0=rrf[:], in1=rr_h[:], op=ALU.subtract)
-        rr_m = const.tile([P, P], BF16, name="rr_m")
-        nc.vector.tensor_copy(out=rr_m[:], in_=rr_d[:])
         rr_w = const.tile([P, P], BF16, name="rr_w")
-        nc.vector.memset(rr_w[:], 0.0)
-        nc.vector.tensor_copy(out=rr_w[0:32, :], in_=rr_h[0:32, :])
-        nc.vector.tensor_copy(out=rr_w[32:64, :], in_=rr_m[32:64, :])
-        nc.vector.tensor_tensor(out=rr_w[64:96, :], in0=rr_d[64:96, :], in1=rr_m[64:96, :], op=ALU.subtract)
+
+        def tables_1():
+            xc_ps = ps_s3.tile([P, 4, P], BF16, name="xc_ps", tag="s3")
+            for t in range(4):
+                nc.tensor.transpose(xc_ps[:, t, :], exc_sb[:, t * P : (t + 1) * P], ident_b[:])
+            rt_ps = ps_s3.tile([P, P], BF16, name="rt_ps", tag="s3")
+            nc.tensor.transpose(rt_ps[:], r_sb[:], ident_b[:])
+            nc.vector.tensor_copy(out=excT[:], in_=xc_ps[:])
+            nc.vector.tensor_copy(out=rTf[:], in_=rt_ps[:])
+            nc.vector.tensor_tensor(out=r2T[:], in0=rTf[:], in1=rTf[:], op=ALU.mult)
+            nc.vector.tensor_scalar(out=rTm2[:], in0=rTf[:], scalar1=-2.0, scalar2=None, op0=ALU.mult)
+
+        def tables_2():
+            ec_ps = ps_s3.tile([P, 4, P], F32, name="ec_ps", tag="s3")
+            for t in range(4):
+                nc.tensor.matmul(out=ec_ps[:, t, :], lhsT=excT[:, t, :], rhs=r_sb[:], start=True, stop=True)
+            rr_ps = ps_s3.tile([P, P], F32, name="rr_ps", tag="s3")
+            nc.tensor.matmul(out=rr_ps[:], lhsT=ones_f[:], rhs=r2T[:], start=True, stop=True)
+            nc.vector.tensor_copy(
+                out=ecg[:].rearrange("p (c t) -> p c t", t=4), in_=ec_ps[:].rearrange("p t c -> p c t")
+            )
+            rrf = const.tile([P, P], F32, name="rrf")
+            nc.vector.tensor_copy(out=rrf[:], in_=rr_ps[:])
+            rr_h = const.tile([P, P], BF16, name="rr_h")
+            nc.vector.tensor_copy(out=rr_h[:], in_=rrf[:])
+            nc.vector.quantize_mx(out=ecr_c[:].bitcast(FP8X4), scales=ecr_s[:], in_=ecg[:])
+            rr_d = const.tile([P, P], F32, name="rr_d")
+            nc.vector.tensor_tensor(out=rr_d[:], in0=rrf[:], in1=rr_h[:], op=ALU.subtract)
+            rr_m = const.tile([P, P], BF16, name="rr_m")
+            nc.vector.tensor_copy(out=rr_m[:], in_=rr_d[:])
+            nc.vector.memset(rr_w[:], 0.0)
+            nc.vector.tensor_copy(out=rr_w[0:32, :], in_=rr_h[0:32, :])
+            nc.vector.tensor_copy(out=rr_w[32:64, :], in_=rr_m[32:64, :])
+            nc.vector.tensor_tensor(
+                out=rr_w[64:96, :], in0=rr_d[64:96, :], in1=rr_m[64:96, :], op=ALU.subtract
+            )
 
         def do_C_pe(m):
             ac, asc = acs[m]
@@ -299,48 +306,72 @@ def tile_minerva_detex_pb_t_kernel(tc, f_n, ex_n, ex_classes, class_reps, out):
                 in_=o[:].rearrange("p (j k) -> p j k", j=4),
             )
 
-        do_T(0)
-        do_T(1)
-        do_E(0, False)
-        do_E(1, True)
-        do_Q(0)
-        do_Q(1)
-        for h in range(N_HALF + 3):
-            i0, i1 = 2 * h, 2 * h + 1
-            n0, n1 = i0 + 2, i1 + 2
-            nxt = n1 < N_TILES
-            cur = i1 < N_TILES
-            mc = (h - 2) // 2 if (h % 2 == 0 and 2 <= h <= N_HALF) else -1
-            md = (h - 3) // 2 if (h % 2 == 1 and 3 <= h) else -1
-            mn = (h - 4) // 2 if (h % 2 == 0 and 4 <= h) else -1
-            if nxt:
-                do_T(n0)
-                do_T(n1)
-                do_E(n0, False)
-                do_E(n1, h % 2 == 1)
-            if mc >= 0:
-                do_C_pe(mc)
-            if cur:
-                do_M(i0)
-                do_M(i1)
-            if mc >= 0:
-                do_C_v(mc)
-                do_C_s(mc)
-            if cur:
-                do_S(i0)
-                do_V(i0)
-            if mn >= 0:
-                do_D_v(mn)
-            if nxt:
-                do_Q(n0)
-            if cur:
-                do_S(i1)
-                do_V(i1)
-                do_QA(i0)
-            if nxt:
-                do_Q(n1)
-            if cur:
-                do_QA(i1)
-            if md >= 0:
-                do_D_pe(md)
-                do_D_s(md)
+        def ok(m):
+            return 0 <= m < N_MACRO
+
+        for j in range(4):
+            do_T(j)
+        for j in range(4):
+            do_E(j, j == 3)
+        for j in range(4):
+            do_Q(j)
+        for m in range(N_MACRO + 2):
+            a, b, c = m - 1, m, m + 1
+            if ok(c):
+                for j in range(4):
+                    do_T(4 * c + j)
+            if ok(a):
+                do_S(4 * a + 3)
+                do_V(4 * a + 3)
+            if ok(c):
+                for j in range(3):
+                    do_E(4 * c + j, False)
+            if ok(a):
+                do_QA(4 * a + 2)
+            if ok(c):
+                do_Q(4 * c)
+            if ok(a):
+                do_QA(4 * a + 3)
+            if ok(c):
+                do_E(4 * c + 3, True)
+            if ok(b):
+                do_M(4 * b)
+            if ok(a):
+                do_C_pe(a)
+            if m == 0:
+                tables_1()
+            if ok(b):
+                do_M(4 * b + 1)
+            if ok(a):
+                do_C_v(a)
+            if ok(b):
+                do_S(4 * b)
+            if ok(a):
+                do_C_s(a)
+                do_D_pe(a)
+            if m == 0:
+                tables_2()
+            if ok(b):
+                do_M(4 * b + 2)
+                do_M(4 * b + 3)
+                do_V(4 * b)
+            if ok(c):
+                do_Q(4 * c + 1)
+            if ok(b):
+                do_QA(4 * b)
+                do_S(4 * b + 1)
+            if ok(a):
+                do_D_s(a)
+            if ok(b):
+                do_V(4 * b + 1)
+            if ok(c):
+                do_Q(4 * c + 2)
+            if ok(b):
+                do_QA(4 * b + 1)
+            if ok(a):
+                do_D_v(a)
+            if ok(c):
+                do_Q(4 * c + 3)
+            if ok(b):
+                do_S(4 * b + 2)
+                do_V(4 * b + 2)

@@ -1,8 +1,6 @@
 from contextlib import ExitStack
 
-import concourse.bass as bass
 import concourse.mybir as mybir
-import concourse.tile as tile
 from concourse.masks import make_identity
 
 F32 = mybir.dt.float32
@@ -18,46 +16,57 @@ B, D, F, C = 8192, 512, 1024, 128
 FLOPS = 2 * B * D * F + 2 * B * D * C + 2 * D * C * C + 3 * B * C * C
 
 MANUAL = True
+XT_BANKS = 2
+ST_BANKS = 4
+NEG_ON_GPSIMD = False
+E_V_EVEN = False
+E_V_ODD = True
 N_TILES = B // P
+N_PAIR = N_TILES // 2
 N_MACRO = N_TILES // 4
-N_HALF = N_TILES // 2
+LAST = N_MACRO - 1
 
 
 def tile_minerva_detex_pb_t_kernel(tc, f_n, ex_n, ex_classes, class_reps, out):
     nc = tc.nc
     with ExitStack() as ctx:
         const = ctx.enter_context(tc.tile_pool(name="const", bufs=1))
-        fpool = ctx.enter_context(tc.tile_pool(name="fpool", bufs=N_MACRO))
-        fgp = ctx.enter_context(tc.tile_pool(name="fgp", bufs=5))
-        fcp = ctx.enter_context(tc.tile_pool(name="fcp", bufs=8))
-        s2p = ctx.enter_context(tc.tile_pool(name="s2p", bufs=3))
-        agp = ctx.enter_context(tc.tile_pool(name="agp", bufs=4))
+        fpool = ctx.enter_context(tc.tile_pool(name="fpool", bufs=N_PAIR))
+        fgp = ctx.enter_context(tc.tile_pool(name="fgp", bufs=4))
+        fcp = ctx.enter_context(tc.tile_pool(name="fcp", bufs=5))
+        s2p = ctx.enter_context(tc.tile_pool(name="s2p", bufs=4))
+        agp = ctx.enter_context(tc.tile_pool(name="agp", bufs=3))
         acp = ctx.enter_context(tc.tile_pool(name="acp", bufs=3))
         e3p = ctx.enter_context(tc.tile_pool(name="e3p", bufs=3))
-        ps_xt = ctx.enter_context(tc.psum_pool(name="ps_xt", bufs=4))
-        ps_st = ctx.enter_context(tc.psum_pool(name="ps_st", bufs=2))
-        ps_s3 = ctx.enter_context(tc.psum_pool(name="ps_s3", bufs=2))
+        psum = ctx.enter_context(tc.psum_pool(name="psum", bufs=1))
+        banks_used = []
+
+        def bank(shape, dtype):
+            n = len(banks_used)
+            banks_used.append(n)
+            return psum.tile(shape, dtype, name="bank%d" % (n % 8), tag="bank%d" % (n % 8))
+
         if MANUAL:
             ctx.enter_context(tc.manual_schedule())
 
+        f_sbs = []
+
+        def load_f(h):
+            f_sb = fpool.tile([P, 2 * F], BF16, name="f_sb", tag="f_sb")
+            nc.sync.dma_start(
+                out=f_sb[:].rearrange("p (i k) -> p i k", i=2),
+                in_=f_n[256 * h : 256 * (h + 1), :].rearrange("(p i) k -> p i k", i=2),
+            )
+            f_sbs.append(f_sb)
+
+        load_f(0)
         ex_rows = ex_n.rearrange("(p t) k -> p t k", t=4)
         ex_sbs = []
         for t in range(4):
             ex_sb = const.tile([P, F], BF16, name="ex_sb%d" % t)
             nc.sync.dma_start(out=ex_sb[:], in_=ex_rows[:, t, :])
             ex_sbs.append(ex_sb)
-        f_tiles = []
-        for m in range(N_MACRO):
-            f_sb = fpool.tile([P, 4 * F], BF16, name="f_sb", tag="f_sb")
-            f_tiles.append(f_sb)
-
-        def load_f(m):
-            nc.sync.dma_start(
-                out=f_tiles[m][:].rearrange("p (j k) -> p j k", j=4),
-                in_=f_n[512 * m : 512 * (m + 1), :].rearrange("(p j) k -> p j k", j=4),
-            )
-
-        load_f(0)
+        load_f(1)
         exc_sb = const.tile([P, 4 * C], BF16, name="exc_sb")
         nc.sync.dma_start(
             out=exc_sb[:].rearrange("p (t j) -> p t j", t=4),
@@ -65,8 +74,8 @@ def tile_minerva_detex_pb_t_kernel(tc, f_n, ex_n, ex_classes, class_reps, out):
         )
         r_sb = const.tile([P, C], BF16, name="r_sb")
         nc.sync.dma_start(out=r_sb[:], in_=class_reps)
-        for m in range(1, N_MACRO):
-            load_f(m)
+        for h in range(2, N_PAIR):
+            load_f(h)
 
         ident = const.tile([P, P], F32, name="ident")
         make_identity(nc, ident[:])
@@ -81,31 +90,6 @@ def tile_minerva_detex_pb_t_kernel(tc, f_n, ex_n, ex_classes, class_reps, out):
         nc.vector.memset(sel[:], 1.0 / 32.0)
         nc.vector.memset(sel[96:128, :], 0.0)
 
-        ex_c = const.tile([P, 4 * 256], U32, name="ex_c", align_bytes=64)
-        ex_s = const.tile([P, 4 * 256], U8, name="ex_s", align_bytes=64)
-        exgs = []
-        for t in range(4):
-            xe = ps_xt.tile([P, 2, 2, P], F32, name="xe", tag="xt")
-            exw = ex_sbs[t][:].bitcast(F32)
-            for g in range(2):
-                for u in range(2):
-                    c0 = 256 * g + 128 * u
-                    nc.tensor.transpose(xe[:, g, u, :], exw[:, c0 : c0 + P], ident[:])
-            exg = const.tile([P, 1024], BF16, name="exg%d" % t, align_bytes=64)
-            dst = exg[:].bitcast(F32).rearrange("p (g b u) -> p g b u", g=2, u=2)
-            src = xe[:].rearrange("p g u b -> p g b u")
-            if t % 2 == 0:
-                nc.vector.tensor_copy(out=dst, in_=src)
-            else:
-                nc.scalar.copy(out=dst, in_=src)
-            exgs.append(exg)
-        for t in range(4):
-            nc.vector.quantize_mx(
-                out=ex_c[:, 256 * t : 256 * (t + 1)].bitcast(FP8X4),
-                scales=ex_s[:, 256 * t : 256 * (t + 1)],
-                in_=exgs[t][:],
-            )
-
         xts = {}
         fgs = {}
         fcs = {}
@@ -115,44 +99,72 @@ def tile_minerva_detex_pb_t_kernel(tc, f_n, ex_n, ex_classes, class_reps, out):
         acs = {}
         c3 = {}
 
-        def do_T(i):
-            m, j = divmod(i, 4)
-            xt = ps_xt.tile([P, 2, 2, P], F32, name="xt", tag="xt")
-            fw = f_tiles[m][:].bitcast(F32)
+        def transposes(bank, words):
             for g in range(2):
                 for u in range(2):
-                    c0 = 512 * j + 256 * g + 128 * u
-                    nc.tensor.transpose(xt[:, g, u, :], fw[:, c0 : c0 + P], ident[:])
-            xts[i] = xt
+                    c0 = 256 * g + 128 * u
+                    nc.tensor.transpose(bank[:, g, u, :], words[:, c0 : c0 + P], ident[:])
 
-        def do_E(i, on_vector):
-            fg = fgp.tile([P, 1024], BF16, name="fg", tag="fg", align_bytes=64)
-            dst = fg[:].bitcast(F32).rearrange("p (g b u) -> p g b u", g=2, u=2)
-            src = xts[i][:].rearrange("p g u b -> p g b u")
+        def copy_out(grouped, bank, on_vector):
+            dst = grouped.bitcast(F32).rearrange("p (g b u) -> p g b u", g=2, u=2)
+            src = bank[:].rearrange("p g u b -> p g b u")
             if on_vector:
                 nc.vector.tensor_copy(out=dst, in_=src)
             else:
                 nc.scalar.copy(out=dst, in_=src)
-            fgs[i] = fg
 
-        def do_Q(i):
-            fc = fcp.tile([P, 256], U32, name="fc", tag="fc", align_bytes=64)
-            fs = fcp.tile([P, 256], U8, name="fs", tag="fs", align_bytes=64)
-            nc.vector.quantize_mx(out=fc[:].bitcast(FP8X4), scales=fs[:], in_=fgs[i][:])
-            fcs[i] = (fc, fs)
+        def do_T(i):
+            h, half = divmod(i, 2)
+            xt = bank([P, 2, 2, P], F32)
+            transposes(xt, f_sbs[h][:].bitcast(F32)[:, 512 * half : 512 * (half + 1)])
+            xts[i] = xt
+
+        def do_E(i, on_vector):
+            h, half = divmod(i, 2)
+            if h not in fgs:
+                fgs[h] = fgp.tile([P, 2048], BF16, name="fg", tag="fg", align_bytes=64)
+            copy_out(fgs[h][:, 1024 * half : 1024 * (half + 1)], xts[i], on_vector)
+
+        def do_Q(h):
+            fc = fcp.tile([P, 512], U32, name="fc", tag="fc", align_bytes=64)
+            fs = fcp.tile([P, 512], U8, name="fs", tag="fs", align_bytes=64)
+            nc.vector.quantize_mx(out=fc[:].bitcast(FP8X4), scales=fs[:], in_=fgs[h][:])
+            fcs[h] = (fc, fs)
+
+        ex_banks = []
+        ex_gs = []
+        ex_cs = []
+
+        def ex_T(t):
+            xe = bank([P, 2, 2, P], F32)
+            transposes(xe, ex_sbs[t][:].bitcast(F32))
+            ex_banks.append(xe)
+
+        def ex_E(t, on_vector):
+            exg = const.tile([P, 1024], BF16, name="exg%d" % t, align_bytes=64)
+            copy_out(exg[:], ex_banks[t], on_vector)
+            ex_gs.append(exg)
+
+        def ex_Q(t):
+            ex_c = const.tile([P, 256], U32, name="ex_c%d" % t, align_bytes=64)
+            ex_s = const.tile([P, 256], U8, name="ex_s%d" % t, align_bytes=64)
+            nc.vector.quantize_mx(out=ex_c[:].bitcast(FP8X4), scales=ex_s[:], in_=ex_gs[t][:])
+            ex_cs.append((ex_c, ex_s))
 
         def do_M(i):
-            fc, fs = fcs[i]
-            st = ps_st.tile([P, 4, P], F32, name="st", tag="st")
+            h, half = divmod(i, 2)
+            fc, fs = fcs[h]
+            st = bank([P, 4, P], F32)
             for t in range(4):
+                ex_c, ex_s = ex_cs[t]
                 for g in range(2):
-                    w0 = (2 * t + g) * P
+                    r0 = (2 * half + g) * P
                     nc.tensor.matmul_mx(
                         out=st[:, t, :],
-                        lhsT=ex_c[:, w0 : w0 + P].bitcast(FP8X4),
-                        lhsT_scale=ex_s[:, w0 : w0 + P],
-                        rhs=fc[:, g * P : (g + 1) * P].bitcast(FP8X4),
-                        rhs_scale=fs[:, g * P : (g + 1) * P],
+                        lhsT=ex_c[:, g * P : (g + 1) * P].bitcast(FP8X4),
+                        lhsT_scale=ex_s[:, g * P : (g + 1) * P],
+                        rhs=fc[:, r0 : r0 + P].bitcast(FP8X4),
+                        rhs_scale=fs[:, r0 : r0 + P],
                         start=(g == 0),
                         stop=(g == 1),
                     )
@@ -168,26 +180,27 @@ def tile_minerva_detex_pb_t_kernel(tc, f_n, ex_n, ex_classes, class_reps, out):
             s2s[i] = s2
 
         def do_V(i):
-            ag = agp.tile([P, 512], BF16, name="ag", tag="ag", align_bytes=64)
+            h, half = divmod(i, 2)
+            if half == 0:
+                ags[h] = agp.tile([P, 1024], BF16, name="ag", tag="ag", align_bytes=64)
             nc.vector.tensor_tensor(
-                out=ag[:].rearrange("p (b t) -> p b t", t=4),
+                out=ags[h][:, 512 * half : 512 * (half + 1)].rearrange("p (b t) -> p b t", t=4),
                 in0=sts[i][:].rearrange("p t b -> p b t"),
                 in1=s2s[i][:].rearrange("p (b t) -> p b t", t=4),
                 op=ALU.mult,
             )
-            ags[i] = ag
 
-        def do_QA(i):
-            m, j = divmod(i, 4)
-            if j == 0:
+        def do_QA(h):
+            m, pair = divmod(h, 2)
+            if pair == 0 or m == LAST:
                 ac = acp.tile([P, 512], U32, name="ac", tag="ac", align_bytes=64)
                 asc = acp.tile([P, 512], U8, name="asc", tag="asc", align_bytes=64)
                 acs[m] = (ac, asc)
             ac, asc = acs[m]
             nc.vector.quantize_mx(
-                out=ac[:, j * P : (j + 1) * P].bitcast(FP8X4),
-                scales=asc[:, j * P : (j + 1) * P],
-                in_=ags[i][:],
+                out=ac[:, 256 * pair : 256 * (pair + 1)].bitcast(FP8X4),
+                scales=asc[:, 256 * pair : 256 * (pair + 1)],
+                in_=ags[h][:],
             )
 
         excT = const.tile([P, 4, P], BF16, name="excT")
@@ -200,10 +213,10 @@ def tile_minerva_detex_pb_t_kernel(tc, f_n, ex_n, ex_classes, class_reps, out):
         rr_w = const.tile([P, P], BF16, name="rr_w")
 
         def tables_1():
-            xc_ps = ps_s3.tile([P, 4, P], BF16, name="xc_ps", tag="s3")
+            xc_ps = bank([P, 4, P], BF16)
             for t in range(4):
                 nc.tensor.transpose(xc_ps[:, t, :], exc_sb[:, t * P : (t + 1) * P], ident_b[:])
-            rt_ps = ps_s3.tile([P, P], BF16, name="rt_ps", tag="s3")
+            rt_ps = bank([P, P], BF16)
             nc.tensor.transpose(rt_ps[:], r_sb[:], ident_b[:])
             nc.vector.tensor_copy(out=excT[:], in_=xc_ps[:])
             nc.vector.tensor_copy(out=rTf[:], in_=rt_ps[:])
@@ -211,10 +224,10 @@ def tile_minerva_detex_pb_t_kernel(tc, f_n, ex_n, ex_classes, class_reps, out):
             nc.vector.tensor_scalar(out=rTm2[:], in0=rTf[:], scalar1=-2.0, scalar2=None, op0=ALU.mult)
 
         def tables_2():
-            ec_ps = ps_s3.tile([P, 4, P], F32, name="ec_ps", tag="s3")
+            ec_ps = bank([P, 4, P], F32)
             for t in range(4):
                 nc.tensor.matmul(out=ec_ps[:, t, :], lhsT=excT[:, t, :], rhs=r_sb[:], start=True, stop=True)
-            rr_ps = ps_s3.tile([P, P], F32, name="rr_ps", tag="s3")
+            rr_ps = bank([P, P], F32)
             nc.tensor.matmul(out=rr_ps[:], lhsT=ones_f[:], rhs=r2T[:], start=True, stop=True)
             nc.vector.tensor_copy(
                 out=ecg[:].rearrange("p (c t) -> p c t", t=4), in_=ec_ps[:].rearrange("p t c -> p c t")
@@ -235,143 +248,171 @@ def tile_minerva_detex_pb_t_kernel(tc, f_n, ex_n, ex_classes, class_reps, out):
                 out=rr_w[64:96, :], in0=rr_d[64:96, :], in1=rr_m[64:96, :], op=ALU.subtract
             )
 
-        def do_C_pe(m):
+        def do_C_pe(m, j0, nj):
             ac, asc = acs[m]
-            eT = ps_s3.tile([P, 512], F32, name="eT", tag="s3")
+            cols = slice(j0 * P, (j0 + nj) * P)
+            eT = bank([P, nj * P], F32)
             nc.tensor.matmul_mx(
                 out=eT[:],
                 lhsT=ecr_c[:].bitcast(FP8X4),
                 lhsT_scale=ecr_s[:],
-                rhs=ac[:].bitcast(FP8X4),
-                rhs_scale=asc[:],
+                rhs=ac[:, cols].bitcast(FP8X4),
+                rhs_scale=asc[:, cols],
                 start=True,
                 stop=True,
             )
-            eb = ps_s3.tile([P, 4, P], F32, name="eb", tag="s3")
-            for j in range(4):
+            eb = bank([P, nj, P], F32)
+            for j in range(nj):
+                jc = slice((j0 + j) * P, (j0 + j + 1) * P)
                 nc.tensor.matmul_mx(
                     out=eb[:, j, :],
-                    lhsT=ac[:, j * P : (j + 1) * P].bitcast(FP8X4),
-                    lhsT_scale=asc[:, j * P : (j + 1) * P],
+                    lhsT=ac[:, jc].bitcast(FP8X4),
+                    lhsT_scale=asc[:, jc],
                     rhs=ecr_c[:].bitcast(FP8X4),
                     rhs_scale=ecr_s[:],
                     start=True,
                     stop=True,
                 )
-            c3[m] = {"eT": eT, "eb": eb}
+            c3[(m, j0)] = {"eT": eT, "eb": eb}
 
-        def do_C_v(m):
-            eTs = e3p.tile([P, 512], F32, name="eTs", tag="eTs")
-            nc.vector.tensor_copy(out=eTs[:], in_=c3[m]["eT"][:])
-            c3[m]["eTs"] = eTs
+        def do_C_v(m, j0, nj):
+            eTs = e3p.tile([P, nj * P], F32, name="eTs", tag="eTs")
+            nc.vector.tensor_copy(out=eTs[:], in_=c3[(m, j0)]["eT"][:])
+            c3[(m, j0)]["eTs"] = eTs
 
-        def do_C_s(m):
-            ee = e3p.tile([P, 4], F32, name="ee", tag="ee")
-            for j in range(4):
+        def do_C_s(m, j0, nj):
+            ee = e3p.tile([P, nj], F32, name="ee", tag="ee")
+            for j in range(nj):
                 junk = e3p.tile([P, P], BF16, name="junk", tag="junk")
                 nc.scalar.activation(
-                    out=junk[:], in_=c3[m]["eb"][:, j, :], func=ACT.Square, accum_out=ee[:, j : j + 1]
+                    out=junk[:], in_=c3[(m, j0)]["eb"][:, j, :], func=ACT.Square, accum_out=ee[:, j : j + 1]
                 )
-            c3[m]["ee"] = ee
+            c3[(m, j0)]["ee"] = ee
 
-        def do_D_pe(m):
-            db = ps_s3.tile([P, 4, P], F32, name="db", tag="s3")
-            eTs = c3[m]["eTs"]
-            for j in range(4):
+        def do_D_pe(m, j0, nj):
+            db = bank([P, nj, P], F32)
+            eTs = c3[(m, j0)]["eTs"]
+            for j in range(nj):
                 nc.tensor.matmul(out=db[:, j, :], lhsT=sel[:], rhs=rr_w[:], start=True, stop=False)
                 nc.tensor.matmul(
                     out=db[:, j, :], lhsT=eTs[:, j * P : (j + 1) * P], rhs=rTm2[:], start=False, stop=True
                 )
-            c3[m]["db"] = db
+            c3[(m, j0)]["db"] = db
 
-        def do_D_s(m):
-            sq = e3p.tile([P, 512], F32, name="sq", tag="sq")
-            for j in range(4):
+        def do_D_s(m, j0, nj):
+            sq = e3p.tile([P, nj * P], F32, name="sq", tag="sq")
+            for j in range(nj):
                 nc.scalar.activation(
                     out=sq[:, j * P : (j + 1) * P],
-                    in_=c3[m]["db"][:, j, :],
+                    in_=c3[(m, j0)]["db"][:, j, :],
                     func=ACT.Sqrt,
-                    bias=c3[m]["ee"][:, j : j + 1],
+                    bias=c3[(m, j0)]["ee"][:, j : j + 1],
                     scale=1.0,
                 )
-            c3[m]["sq"] = sq
+            c3[(m, j0)]["sq"] = sq
 
-        def do_D_v(m):
-            o = e3p.tile([P, 512], F32, name="o", tag="o")
-            nc.vector.tensor_scalar(
-                out=o[:], in0=c3[m]["sq"][:], scalar1=-1.0, scalar2=0.0, op0=ALU.mult, op1=ALU.min
+        def do_D_v(m, j0, nj):
+            o = e3p.tile([P, nj * P], F32, name="o", tag="o")
+            eng = nc.gpsimd if NEG_ON_GPSIMD else nc.vector
+            eng.tensor_scalar(
+                out=o[:], in0=c3[(m, j0)]["sq"][:], scalar1=-1.0, scalar2=0.0, op0=ALU.mult, op1=ALU.min
             )
+            r0 = 512 * m + P * j0
             nc.sync.dma_start(
-                out=out[512 * m : 512 * (m + 1), :].rearrange("(p j) k -> p j k", j=4),
-                in_=o[:].rearrange("p (j k) -> p j k", j=4),
+                out=out[r0 : r0 + nj * P, :].rearrange("(q p i) k -> p q i k", p=P, i=2),
+                in_=o[:].rearrange("p (q i k) -> p q i k", i=2, k=C),
             )
+
+        do_T(0)
+        do_T(1)
+        do_E(0, False)
+        do_E(1, True)
+        for t in range(4):
+            ex_T(t)
+        ex_E(0, False)
+        ex_E(1, True)
+        do_Q(0)
+        ex_Q(0)
+        ex_E(2, False)
+        ex_E(3, True)
+        ex_Q(1)
+        do_T(2)
+        do_T(3)
+        ex_Q(2)
+        ex_Q(3)
+        do_E(2, False)
+        do_E(3, True)
 
         def ok(m):
             return 0 <= m < N_MACRO
 
-        for j in range(4):
-            do_T(j)
-        for j in range(4):
-            do_E(j, j == 3)
-        for j in range(4):
-            do_Q(j)
-        for m in range(N_MACRO + 2):
-            a, b, c = m - 1, m, m + 1
+        def mid(m):
+            return 0 <= m < LAST
+
+        do_M(0)
+        do_M(1)
+        for m in range(N_MACRO + 1):
+            z, a, b, c = m - 2, m - 1, m, m + 1
             if ok(c):
                 for j in range(4):
                     do_T(4 * c + j)
+            if a == LAST:
+                do_C_pe(a, 0, 2)
+            if mid(z):
+                do_D_s(z, 0, 4)
             if ok(a):
-                do_S(4 * a + 3)
                 do_V(4 * a + 3)
-            if ok(c):
-                for j in range(3):
-                    do_E(4 * c + j, False)
+            if ok(b):
+                do_Q(2 * b + 1)
+            if a == LAST:
+                do_C_v(a, 0, 2)
             if ok(a):
-                do_QA(4 * a + 2)
+                do_QA(2 * a + 1)
             if ok(c):
-                do_Q(4 * c)
-            if ok(a):
-                do_QA(4 * a + 3)
+                do_E(4 * c, False)
+                do_E(4 * c + 1, False)
+            if mid(z):
+                do_D_v(z, 0, 4)
             if ok(c):
                 do_E(4 * c + 3, True)
-            if ok(b):
+            if ok(b) and m > 0:
                 do_M(4 * b)
-            if ok(a):
-                do_C_pe(a)
+                do_M(4 * b + 1)
             if m == 0:
                 tables_1()
-            if ok(b):
-                do_M(4 * b + 1)
-            if ok(a):
-                do_C_v(a)
+            if mid(a):
+                do_C_pe(a, 0, 4)
+            if ok(c):
+                do_Q(2 * c)
             if ok(b):
                 do_S(4 * b)
-            if ok(a):
-                do_C_s(a)
-                do_D_pe(a)
-            if m == 0:
-                tables_2()
+                do_S(4 * b + 1)
+            if mid(a):
+                do_C_v(a, 0, 4)
             if ok(b):
+                do_V(4 * b)
+                do_V(4 * b + 1)
                 do_M(4 * b + 2)
                 do_M(4 * b + 3)
-                do_V(4 * b)
+            if m == 0:
+                tables_2()
             if ok(c):
-                do_Q(4 * c + 1)
-            if ok(b):
-                do_QA(4 * b)
-                do_S(4 * b + 1)
-            if ok(a):
-                do_D_s(a)
-            if ok(b):
-                do_V(4 * b + 1)
-            if ok(c):
-                do_Q(4 * c + 2)
-            if ok(b):
-                do_QA(4 * b + 1)
-            if ok(a):
-                do_D_v(a)
-            if ok(c):
-                do_Q(4 * c + 3)
+                do_E(4 * c + 2, False)
+            if mid(a):
+                do_C_s(a, 0, 4)
+                do_D_pe(a, 0, 4)
             if ok(b):
                 do_S(4 * b + 2)
+                do_S(4 * b + 3)
                 do_V(4 * b + 2)
+                do_QA(2 * b)
+        do_C_s(LAST, 0, 2)
+        do_C_pe(LAST, 2, 2)
+        do_D_pe(LAST, 0, 2)
+        do_C_v(LAST, 2, 2)
+        do_C_s(LAST, 2, 2)
+        do_D_s(LAST, 0, 2)
+        do_D_pe(LAST, 2, 2)
+        do_D_v(LAST, 0, 2)
+        do_D_s(LAST, 2, 2)
+        do_D_v(LAST, 2, 2)

@@ -18,7 +18,7 @@ FLOPS = 2 * B * D * F + 2 * B * D * C + 2 * D * C * C + 3 * B * C * C
 MANUAL = True
 XT_BANKS = 2
 ST_BANKS = 4
-NEG_ON_GPSIMD = False
+NEG_ON_GPSIMD = True
 E_V_EVEN = False
 E_V_ODD = True
 N_TILES = B // P
@@ -349,8 +349,15 @@ def tile_minerva_detex_pb_t_kernel(tc, f_n, ex_n, ex_classes, class_reps, out):
         def mid(m):
             return 0 <= m < LAST
 
+        def E2_ON_V(m):
+            return True
+
         do_M(0)
         do_M(1)
+        do_S(0)
+        do_S(1)
+        do_V(0)
+        do_V(1)
         for m in range(N_MACRO + 1):
             z, a, b, c = m - 2, m - 1, m, m + 1
             if ok(c):
@@ -374,6 +381,8 @@ def tile_minerva_detex_pb_t_kernel(tc, f_n, ex_n, ex_classes, class_reps, out):
             if mid(z):
                 do_D_v(z, 0, 4)
             if ok(c):
+                if E2_ON_V(m):
+                    do_E(4 * c + 2, True)
                 do_E(4 * c + 3, True)
             if ok(b) and m > 0:
                 do_M(4 * b)
@@ -384,26 +393,31 @@ def tile_minerva_detex_pb_t_kernel(tc, f_n, ex_n, ex_classes, class_reps, out):
                 do_C_pe(a, 0, 4)
             if ok(c):
                 do_Q(2 * c)
-            if ok(b):
+            if ok(b) and m > 0:
                 do_S(4 * b)
                 do_S(4 * b + 1)
             if mid(a):
                 do_C_v(a, 0, 4)
-            if ok(b):
+            if ok(b) and m > 0:
                 do_V(4 * b)
                 do_V(4 * b + 1)
+            if ok(b):
                 do_M(4 * b + 2)
                 do_M(4 * b + 3)
             if m == 0:
                 tables_2()
-            if ok(c):
+            if ok(c) and not E2_ON_V(m):
                 do_E(4 * c + 2, False)
+            if b == LAST:
+                do_S(4 * b + 2)
+                do_S(4 * b + 3)
             if mid(a):
                 do_C_s(a, 0, 4)
                 do_D_pe(a, 0, 4)
-            if ok(b):
+            if mid(b):
                 do_S(4 * b + 2)
                 do_S(4 * b + 3)
+            if ok(b):
                 do_V(4 * b + 2)
                 do_QA(2 * b)
         do_C_s(LAST, 0, 2)

@@ -15,12 +15,11 @@ P = 128
 B, D, F, C = 8192, 512, 1024, 128
 FLOPS = 2 * B * D * F + 2 * B * D * C + 2 * D * C * C + 3 * B * C * C
 
-MANUAL = True
+MANUAL = False
 XT_BANKS = 2
 ST_BANKS = 4
-NEG_ON_GPSIMD = True
-E_V_EVEN = False
-E_V_ODD = True
+NEG_ON_GPSIMD = False
+E3_ON_V = False
 N_TILES = B // P
 N_PAIR = N_TILES // 2
 N_MACRO = N_TILES // 4
@@ -37,7 +36,7 @@ def tile_minerva_detex_pb_t_kernel(tc, f_n, ex_n, ex_classes, class_reps, out):
         s2p = ctx.enter_context(tc.tile_pool(name="s2p", bufs=4))
         agp = ctx.enter_context(tc.tile_pool(name="agp", bufs=3))
         acp = ctx.enter_context(tc.tile_pool(name="acp", bufs=3))
-        e3p = ctx.enter_context(tc.tile_pool(name="e3p", bufs=3))
+        e3p = ctx.enter_context(tc.tile_pool(name="e3p", bufs=2))
         psum = ctx.enter_context(tc.psum_pool(name="psum", bufs=1))
         banks_used = []
 
@@ -86,9 +85,6 @@ def tile_minerva_detex_pb_t_kernel(tc, f_n, ex_n, ex_classes, class_reps, out):
         nc.scalar.activation(out=warm[:], in_=warm[:], func=ACT.Sqrt)
         ones_f = const.tile([P, P], F32, name="ones_f")
         nc.vector.memset(ones_f[:], 1.0)
-        sel = const.tile([P, P], BF16, name="sel")
-        nc.vector.memset(sel[:], 1.0 / 32.0)
-        nc.vector.memset(sel[96:128, :], 0.0)
 
         xts = {}
         fgs = {}
@@ -210,7 +206,7 @@ def tile_minerva_detex_pb_t_kernel(tc, f_n, ex_n, ex_classes, class_reps, out):
         ecr_s = const.tile([P, P], U8, name="ecr_s", align_bytes=64)
         rTm2 = const.tile([P, P], F32, name="rTm2")
         r2T = const.tile([P, P], F32, name="r2T")
-        rr_w = const.tile([P, P], BF16, name="rr_w")
+        rrf = const.tile([P, P], F32, name="rrf")
 
         def tables_1():
             xc_ps = bank([P, 4, P], BF16)
@@ -232,21 +228,8 @@ def tile_minerva_detex_pb_t_kernel(tc, f_n, ex_n, ex_classes, class_reps, out):
             nc.vector.tensor_copy(
                 out=ecg[:].rearrange("p (c t) -> p c t", t=4), in_=ec_ps[:].rearrange("p t c -> p c t")
             )
-            rrf = const.tile([P, P], F32, name="rrf")
             nc.vector.tensor_copy(out=rrf[:], in_=rr_ps[:])
-            rr_h = const.tile([P, P], BF16, name="rr_h")
-            nc.vector.tensor_copy(out=rr_h[:], in_=rrf[:])
             nc.vector.quantize_mx(out=ecr_c[:].bitcast(FP8X4), scales=ecr_s[:], in_=ecg[:])
-            rr_d = const.tile([P, P], F32, name="rr_d")
-            nc.vector.tensor_tensor(out=rr_d[:], in0=rrf[:], in1=rr_h[:], op=ALU.subtract)
-            rr_m = const.tile([P, P], BF16, name="rr_m")
-            nc.vector.tensor_copy(out=rr_m[:], in_=rr_d[:])
-            nc.vector.memset(rr_w[:], 0.0)
-            nc.vector.tensor_copy(out=rr_w[0:32, :], in_=rr_h[0:32, :])
-            nc.vector.tensor_copy(out=rr_w[32:64, :], in_=rr_m[32:64, :])
-            nc.vector.tensor_tensor(
-                out=rr_w[64:96, :], in0=rr_d[64:96, :], in1=rr_m[64:96, :], op=ALU.subtract
-            )
 
         def do_C_pe(m, j0, nj):
             ac, asc = acs[m]
@@ -293,22 +276,27 @@ def tile_minerva_detex_pb_t_kernel(tc, f_n, ex_n, ex_classes, class_reps, out):
             db = bank([P, nj, P], F32)
             eTs = c3[(m, j0)]["eTs"]
             for j in range(nj):
-                nc.tensor.matmul(out=db[:, j, :], lhsT=sel[:], rhs=rr_w[:], start=True, stop=False)
                 nc.tensor.matmul(
-                    out=db[:, j, :], lhsT=eTs[:, j * P : (j + 1) * P], rhs=rTm2[:], start=False, stop=True
+                    out=db[:, j, :], lhsT=eTs[:, j * P : (j + 1) * P], rhs=rTm2[:], start=True, stop=True
                 )
             c3[(m, j0)]["db"] = db
 
+        def do_D_y(m, j0, nj):
+            y = e3p.tile([P, nj * P], F32, name="y", tag="y")
+            for j in range(nj):
+                nc.vector.scalar_tensor_tensor(
+                    out=y[:, j * P : (j + 1) * P],
+                    in0=c3[(m, j0)]["db"][:, j, :],
+                    scalar=c3[(m, j0)]["ee"][:, j : j + 1],
+                    in1=rrf[:],
+                    op0=ALU.add,
+                    op1=ALU.add,
+                )
+            c3[(m, j0)]["y"] = y
+
         def do_D_s(m, j0, nj):
             sq = e3p.tile([P, nj * P], F32, name="sq", tag="sq")
-            for j in range(nj):
-                nc.scalar.activation(
-                    out=sq[:, j * P : (j + 1) * P],
-                    in_=c3[(m, j0)]["db"][:, j, :],
-                    func=ACT.Sqrt,
-                    bias=c3[(m, j0)]["ee"][:, j : j + 1],
-                    scale=1.0,
-                )
+            nc.scalar.activation(out=sq[:], in_=c3[(m, j0)]["y"][:], func=ACT.Sqrt)
             c3[(m, j0)]["sq"] = sq
 
         def do_D_v(m, j0, nj):
@@ -349,9 +337,6 @@ def tile_minerva_detex_pb_t_kernel(tc, f_n, ex_n, ex_classes, class_reps, out):
         def mid(m):
             return 0 <= m < LAST
 
-        def E2_ON_V(m):
-            return True
-
         do_M(0)
         do_M(1)
         do_S(0)
@@ -366,7 +351,7 @@ def tile_minerva_detex_pb_t_kernel(tc, f_n, ex_n, ex_classes, class_reps, out):
             if a == LAST:
                 do_C_pe(a, 0, 2)
             if mid(z):
-                do_D_s(z, 0, 4)
+                do_D_y(z, 0, 4)
             if ok(a):
                 do_V(4 * a + 3)
             if ok(b):
@@ -379,10 +364,8 @@ def tile_minerva_detex_pb_t_kernel(tc, f_n, ex_n, ex_classes, class_reps, out):
                 do_E(4 * c, False)
                 do_E(4 * c + 1, False)
             if mid(z):
-                do_D_v(z, 0, 4)
-            if ok(c):
-                if E2_ON_V(m):
-                    do_E(4 * c + 2, True)
+                do_D_s(z, 0, 4)
+            if ok(c) and E3_ON_V:
                 do_E(4 * c + 3, True)
             if ok(b) and m > 0:
                 do_M(4 * b)
@@ -398,6 +381,8 @@ def tile_minerva_detex_pb_t_kernel(tc, f_n, ex_n, ex_classes, class_reps, out):
                 do_S(4 * b + 1)
             if mid(a):
                 do_C_v(a, 0, 4)
+            if mid(z):
+                do_D_v(z, 0, 4)
             if ok(b) and m > 0:
                 do_V(4 * b)
                 do_V(4 * b + 1)
@@ -406,8 +391,10 @@ def tile_minerva_detex_pb_t_kernel(tc, f_n, ex_n, ex_classes, class_reps, out):
                 do_M(4 * b + 3)
             if m == 0:
                 tables_2()
-            if ok(c) and not E2_ON_V(m):
+            if ok(c):
                 do_E(4 * c + 2, False)
+                if not E3_ON_V:
+                    do_E(4 * c + 3, False)
             if b == LAST:
                 do_S(4 * b + 2)
                 do_S(4 * b + 3)
@@ -425,8 +412,10 @@ def tile_minerva_detex_pb_t_kernel(tc, f_n, ex_n, ex_classes, class_reps, out):
         do_D_pe(LAST, 0, 2)
         do_C_v(LAST, 2, 2)
         do_C_s(LAST, 2, 2)
+        do_D_y(LAST, 0, 2)
         do_D_s(LAST, 0, 2)
         do_D_pe(LAST, 2, 2)
         do_D_v(LAST, 0, 2)
+        do_D_y(LAST, 2, 2)
         do_D_s(LAST, 2, 2)
         do_D_v(LAST, 2, 2)

@@ -15,11 +15,12 @@ P = 128
 B, D, F, C = 8192, 512, 1024, 128
 FLOPS = 2 * B * D * F + 2 * B * D * C + 2 * D * C * C + 3 * B * C * C
 
-MANUAL = False
+MANUAL = True
 XT_BANKS = 2
 ST_BANKS = 4
 NEG_ON_GPSIMD = False
-E3_ON_V = False
+E_V_EVEN = False
+E_V_ODD = True
 N_TILES = B // P
 N_PAIR = N_TILES // 2
 N_MACRO = N_TILES // 4
@@ -36,7 +37,7 @@ def tile_minerva_detex_pb_t_kernel(tc, f_n, ex_n, ex_classes, class_reps, out):
         s2p = ctx.enter_context(tc.tile_pool(name="s2p", bufs=4))
         agp = ctx.enter_context(tc.tile_pool(name="agp", bufs=3))
         acp = ctx.enter_context(tc.tile_pool(name="acp", bufs=3))
-        e3p = ctx.enter_context(tc.tile_pool(name="e3p", bufs=2))
+        e3p = ctx.enter_context(tc.tile_pool(name="e3p", bufs=3))
         psum = ctx.enter_context(tc.psum_pool(name="psum", bufs=1))
         banks_used = []
 
@@ -85,6 +86,9 @@ def tile_minerva_detex_pb_t_kernel(tc, f_n, ex_n, ex_classes, class_reps, out):
         nc.scalar.activation(out=warm[:], in_=warm[:], func=ACT.Sqrt)
         ones_f = const.tile([P, P], F32, name="ones_f")
         nc.vector.memset(ones_f[:], 1.0)
+        sel = const.tile([P, P], BF16, name="sel")
+        nc.vector.memset(sel[:], 1.0 / 32.0)
+        nc.vector.memset(sel[96:128, :], 0.0)
 
         xts = {}
         fgs = {}
@@ -191,8 +195,8 @@ def tile_minerva_detex_pb_t_kernel(tc, f_n, ex_n, ex_classes, class_reps, out):
             if pair == 0 or m == LAST:
                 ac = acp.tile([P, 512], U32, name="ac", tag="ac", align_bytes=64)
                 asc = acp.tile([P, 512], U8, name="asc", tag="asc", align_bytes=64)
-                acs[m] = (ac, asc)
-            ac, asc = acs[m]
+                acs[(m, pair)] = (ac, asc)
+            ac, asc = acs[(m, pair if m == LAST else 0)]
             nc.vector.quantize_mx(
                 out=ac[:, 256 * pair : 256 * (pair + 1)].bitcast(FP8X4),
                 scales=asc[:, 256 * pair : 256 * (pair + 1)],
@@ -206,7 +210,7 @@ def tile_minerva_detex_pb_t_kernel(tc, f_n, ex_n, ex_classes, class_reps, out):
         ecr_s = const.tile([P, P], U8, name="ecr_s", align_bytes=64)
         rTm2 = const.tile([P, P], F32, name="rTm2")
         r2T = const.tile([P, P], F32, name="r2T")
-        rrf = const.tile([P, P], F32, name="rrf")
+        rr_w = const.tile([P, P], BF16, name="rr_w")
 
         def tables_1():
             xc_ps = bank([P, 4, P], BF16)
@@ -228,11 +232,24 @@ def tile_minerva_detex_pb_t_kernel(tc, f_n, ex_n, ex_classes, class_reps, out):
             nc.vector.tensor_copy(
                 out=ecg[:].rearrange("p (c t) -> p c t", t=4), in_=ec_ps[:].rearrange("p t c -> p c t")
             )
+            rrf = const.tile([P, P], F32, name="rrf")
             nc.vector.tensor_copy(out=rrf[:], in_=rr_ps[:])
+            rr_h = const.tile([P, P], BF16, name="rr_h")
+            nc.vector.tensor_copy(out=rr_h[:], in_=rrf[:])
             nc.vector.quantize_mx(out=ecr_c[:].bitcast(FP8X4), scales=ecr_s[:], in_=ecg[:])
+            rr_d = const.tile([P, P], F32, name="rr_d")
+            nc.vector.tensor_tensor(out=rr_d[:], in0=rrf[:], in1=rr_h[:], op=ALU.subtract)
+            rr_m = const.tile([P, P], BF16, name="rr_m")
+            nc.vector.tensor_copy(out=rr_m[:], in_=rr_d[:])
+            nc.vector.memset(rr_w[:], 0.0)
+            nc.vector.tensor_copy(out=rr_w[0:32, :], in_=rr_h[0:32, :])
+            nc.vector.tensor_copy(out=rr_w[32:64, :], in_=rr_m[32:64, :])
+            nc.vector.tensor_tensor(
+                out=rr_w[64:96, :], in0=rr_d[64:96, :], in1=rr_m[64:96, :], op=ALU.subtract
+            )
 
         def do_C_pe(m, j0, nj):
-            ac, asc = acs[m]
+            ac, asc = acs[(m, j0 // 2)]
             cols = slice(j0 * P, (j0 + nj) * P)
             eT = bank([P, nj * P], F32)
             nc.tensor.matmul_mx(
@@ -276,27 +293,22 @@ def tile_minerva_detex_pb_t_kernel(tc, f_n, ex_n, ex_classes, class_reps, out):
             db = bank([P, nj, P], F32)
             eTs = c3[(m, j0)]["eTs"]
             for j in range(nj):
+                nc.tensor.matmul(out=db[:, j, :], lhsT=sel[:], rhs=rr_w[:], start=True, stop=False)
                 nc.tensor.matmul(
-                    out=db[:, j, :], lhsT=eTs[:, j * P : (j + 1) * P], rhs=rTm2[:], start=True, stop=True
+                    out=db[:, j, :], lhsT=eTs[:, j * P : (j + 1) * P], rhs=rTm2[:], start=False, stop=True
                 )
             c3[(m, j0)]["db"] = db
 
-        def do_D_y(m, j0, nj):
-            y = e3p.tile([P, nj * P], F32, name="y", tag="y")
-            for j in range(nj):
-                nc.vector.scalar_tensor_tensor(
-                    out=y[:, j * P : (j + 1) * P],
-                    in0=c3[(m, j0)]["db"][:, j, :],
-                    scalar=c3[(m, j0)]["ee"][:, j : j + 1],
-                    in1=rrf[:],
-                    op0=ALU.add,
-                    op1=ALU.add,
-                )
-            c3[(m, j0)]["y"] = y
-
         def do_D_s(m, j0, nj):
             sq = e3p.tile([P, nj * P], F32, name="sq", tag="sq")
-            nc.scalar.activation(out=sq[:], in_=c3[(m, j0)]["y"][:], func=ACT.Sqrt)
+            for j in range(nj):
+                nc.scalar.activation(
+                    out=sq[:, j * P : (j + 1) * P],
+                    in_=c3[(m, j0)]["db"][:, j, :],
+                    func=ACT.Sqrt,
+                    bias=c3[(m, j0)]["ee"][:, j : j + 1],
+                    scale=1.0,
+                )
             c3[(m, j0)]["sq"] = sq
 
         def do_D_v(m, j0, nj):
@@ -343,30 +355,28 @@ def tile_minerva_detex_pb_t_kernel(tc, f_n, ex_n, ex_classes, class_reps, out):
         do_S(1)
         do_V(0)
         do_V(1)
-        for m in range(N_MACRO + 1):
-            z, a, b, c = m - 2, m - 1, m, m + 1
+        for m in range(N_MACRO + 2):
+            y, z, a, b, c = m - 3, m - 2, m - 1, m, m + 1
             if ok(c):
                 for j in range(4):
                     do_T(4 * c + j)
-            if a == LAST:
-                do_C_pe(a, 0, 2)
             if mid(z):
-                do_D_y(z, 0, 4)
+                do_D_pe(z, 0, 4)
             if ok(a):
+                do_S(4 * a + 3)
+            if ok(c):
+                do_E(4 * c, False)
+            if ok(a):
+                do_V(4 * a + 2)
                 do_V(4 * a + 3)
             if ok(b):
                 do_Q(2 * b + 1)
-            if a == LAST:
-                do_C_v(a, 0, 2)
             if ok(a):
                 do_QA(2 * a + 1)
             if ok(c):
-                do_E(4 * c, False)
                 do_E(4 * c + 1, False)
-            if mid(z):
-                do_D_s(z, 0, 4)
-            if ok(c) and E3_ON_V:
                 do_E(4 * c + 3, True)
+                do_E(4 * c + 2, False)
             if ok(b) and m > 0:
                 do_M(4 * b)
                 do_M(4 * b + 1)
@@ -374,48 +384,39 @@ def tile_minerva_detex_pb_t_kernel(tc, f_n, ex_n, ex_classes, class_reps, out):
                 tables_1()
             if mid(a):
                 do_C_pe(a, 0, 4)
+            if mid(z):
+                do_D_s(z, 0, 4)
             if ok(c):
                 do_Q(2 * c)
-            if ok(b) and m > 0:
-                do_S(4 * b)
-                do_S(4 * b + 1)
-            if mid(a):
-                do_C_v(a, 0, 4)
             if mid(z):
                 do_D_v(z, 0, 4)
             if ok(b) and m > 0:
+                do_S(4 * b)
                 do_V(4 * b)
-                do_V(4 * b + 1)
+                do_S(4 * b + 1)
             if ok(b):
                 do_M(4 * b + 2)
                 do_M(4 * b + 3)
             if m == 0:
                 tables_2()
-            if ok(c):
-                do_E(4 * c + 2, False)
-                if not E3_ON_V:
-                    do_E(4 * c + 3, False)
-            if b == LAST:
-                do_S(4 * b + 2)
-                do_S(4 * b + 3)
+            if ok(b) and m > 0:
+                do_V(4 * b + 1)
             if mid(a):
+                do_C_v(a, 0, 4)
                 do_C_s(a, 0, 4)
-                do_D_pe(a, 0, 4)
-            if mid(b):
-                do_S(4 * b + 2)
-                do_S(4 * b + 3)
             if ok(b):
-                do_V(4 * b + 2)
                 do_QA(2 * b)
-        do_C_s(LAST, 0, 2)
-        do_C_pe(LAST, 2, 2)
-        do_D_pe(LAST, 0, 2)
-        do_C_v(LAST, 2, 2)
-        do_C_s(LAST, 2, 2)
-        do_D_y(LAST, 0, 2)
-        do_D_s(LAST, 0, 2)
-        do_D_pe(LAST, 2, 2)
-        do_D_v(LAST, 0, 2)
-        do_D_y(LAST, 2, 2)
-        do_D_s(LAST, 2, 2)
-        do_D_v(LAST, 2, 2)
+                do_S(4 * b + 2)
+            if a == LAST:
+                do_C_pe(LAST, 0, 2)
+                do_C_v(LAST, 0, 2)
+                do_C_s(LAST, 0, 2)
+                do_C_pe(LAST, 2, 2)
+                do_D_pe(LAST, 0, 2)
+                do_C_v(LAST, 2, 2)
+                do_C_s(LAST, 2, 2)
+                do_D_s(LAST, 0, 2)
+                do_D_pe(LAST, 2, 2)
+                do_D_v(LAST, 0, 2)
+                do_D_s(LAST, 2, 2)
+                do_D_v(LAST, 2, 2)

@@ -208,7 +208,7 @@ def tile_minerva_detex_pb_t_kernel(tc, f_n, ex_n, ex_classes, class_reps, out):
         ecg = const.tile([P, 512], BF16, name="ecg", align_bytes=64)
         ecr_c = const.tile([P, P], U32, name="ecr_c", align_bytes=64)
         ecr_s = const.tile([P, P], U8, name="ecr_s", align_bytes=64)
-        rTm2 = const.tile([P, P], F32, name="rTm2")
+        rTm2 = const.tile([P, P], BF16, name="rTm2")
         r2T = const.tile([P, P], F32, name="r2T")
         rr_w = const.tile([P, P], BF16, name="rr_w")
 
@@ -276,9 +276,14 @@ def tile_minerva_detex_pb_t_kernel(tc, f_n, ex_n, ex_classes, class_reps, out):
             c3[(m, j0)] = {"eT": eT, "eb": eb}
 
         def do_C_v(m, j0, nj):
-            eTs = e3p.tile([P, nj * P], F32, name="eTs", tag="eTs")
-            nc.vector.tensor_copy(out=eTs[:], in_=c3[(m, j0)]["eT"][:])
-            c3[(m, j0)]["eTs"] = eTs
+            em = e3p.tile([P, nj * P], BF16, name="em", tag="em")
+            nc.vector.tensor_tensor(out=em[:], in0=c3[(m, j0)]["eT"][:], in1=c3[(m, j0)]["eh"][:], op=ALU.subtract)
+            c3[(m, j0)]["em"] = em
+
+        def do_C_h(m, j0, nj):
+            eh = e3p.tile([P, nj * P], BF16, name="eh", tag="eh")
+            nc.scalar.copy(out=eh[:], in_=c3[(m, j0)]["eT"][:])
+            c3[(m, j0)]["eh"] = eh
 
         def do_C_s(m, j0, nj):
             ee = e3p.tile([P, nj], F32, name="ee", tag="ee")
@@ -291,12 +296,12 @@ def tile_minerva_detex_pb_t_kernel(tc, f_n, ex_n, ex_classes, class_reps, out):
 
         def do_D_pe(m, j0, nj):
             db = bank([P, nj, P], F32)
-            eTs = c3[(m, j0)]["eTs"]
+            eh, em = c3[(m, j0)]["eh"], c3[(m, j0)]["em"]
             for j in range(nj):
+                jc = slice(j * P, (j + 1) * P)
                 nc.tensor.matmul(out=db[:, j, :], lhsT=sel[:], rhs=rr_w[:], start=True, stop=False)
-                nc.tensor.matmul(
-                    out=db[:, j, :], lhsT=eTs[:, j * P : (j + 1) * P], rhs=rTm2[:], start=False, stop=True
-                )
+                nc.tensor.matmul(out=db[:, j, :], lhsT=em[:, jc], rhs=rTm2[:], start=False, stop=False)
+                nc.tensor.matmul(out=db[:, j, :], lhsT=eh[:, jc], rhs=rTm2[:], start=False, stop=True)
             c3[(m, j0)]["db"] = db
 
         def do_D_s(m, j0, nj):
@@ -402,6 +407,7 @@ def tile_minerva_detex_pb_t_kernel(tc, f_n, ex_n, ex_classes, class_reps, out):
             if ok(b) and m > 0:
                 do_V(4 * b + 1)
             if mid(a):
+                do_C_h(a, 0, 4)
                 do_C_v(a, 0, 4)
                 do_C_s(a, 0, 4)
             if ok(b):
@@ -409,9 +415,11 @@ def tile_minerva_detex_pb_t_kernel(tc, f_n, ex_n, ex_classes, class_reps, out):
                 do_S(4 * b + 2)
             if a == LAST:
                 do_C_pe(LAST, 0, 2)
+                do_C_h(LAST, 0, 2)
                 do_C_v(LAST, 0, 2)
                 do_C_s(LAST, 0, 2)
                 do_C_pe(LAST, 2, 2)
+                do_C_h(LAST, 2, 2)
                 do_D_pe(LAST, 0, 2)
                 do_C_v(LAST, 2, 2)
                 do_C_s(LAST, 2, 2)

@@ -23,6 +23,7 @@ E_V_EVEN = False
 E_V_ODD = True
 N_TILES = B // P
 N_PAIR = N_TILES // 2
+PREFETCH = 5
 N_MACRO = N_TILES // 4
 LAST = N_MACRO - 1
 
@@ -67,6 +68,8 @@ def tile_minerva_detex_pb_t_kernel(tc, f_n, ex_n, ex_classes, class_reps, out):
             nc.sync.dma_start(out=ex_sb[:], in_=ex_rows[:, t, :])
             ex_sbs.append(ex_sb)
         load_f(1)
+        load_f(2)
+        load_f(3)
         exc_sb = const.tile([P, 4 * C], BF16, name="exc_sb")
         nc.sync.dma_start(
             out=exc_sb[:].rearrange("p (t j) -> p t j", t=4),
@@ -74,7 +77,7 @@ def tile_minerva_detex_pb_t_kernel(tc, f_n, ex_n, ex_classes, class_reps, out):
         )
         r_sb = const.tile([P, C], BF16, name="r_sb")
         nc.sync.dma_start(out=r_sb[:], in_=class_reps)
-        for h in range(2, N_PAIR):
+        for h in range(4, 2 * PREFETCH):
             load_f(h)
 
         ident = const.tile([P, P], F32, name="ident")
@@ -84,11 +87,11 @@ def tile_minerva_detex_pb_t_kernel(tc, f_n, ex_n, ex_classes, class_reps, out):
         warm = const.tile([P, 1], F32, name="warm")
         nc.vector.memset(warm[:], 1.0)
         nc.scalar.activation(out=warm[:], in_=warm[:], func=ACT.Sqrt)
-        ones_f = const.tile([P, P], F32, name="ones_f")
-        nc.vector.memset(ones_f[:], 1.0)
+        quarter = const.tile([P, P], F32, name="quarter")
+        nc.gpsimd.memset(quarter[:], 0.25)
         sel = const.tile([P, P], BF16, name="sel")
-        nc.vector.memset(sel[:], 1.0 / 32.0)
-        nc.vector.memset(sel[96:128, :], 0.0)
+        nc.gpsimd.memset(sel[:], 1.0 / 32.0)
+        nc.gpsimd.memset(sel[96:128, :], 0.0)
 
         xts = {}
         fgs = {}
@@ -204,7 +207,6 @@ def tile_minerva_detex_pb_t_kernel(tc, f_n, ex_n, ex_classes, class_reps, out):
             )
 
         excT = const.tile([P, 4, P], BF16, name="excT")
-        rTf = const.tile([P, P], F32, name="rTf")
         ecg = const.tile([P, 512], BF16, name="ecg", align_bytes=64)
         ecr_c = const.tile([P, P], U32, name="ecr_c", align_bytes=64)
         ecr_s = const.tile([P, P], U8, name="ecr_s", align_bytes=64)
@@ -219,32 +221,38 @@ def tile_minerva_detex_pb_t_kernel(tc, f_n, ex_n, ex_classes, class_reps, out):
             rt_ps = bank([P, P], BF16)
             nc.tensor.transpose(rt_ps[:], r_sb[:], ident_b[:])
             nc.vector.tensor_copy(out=excT[:], in_=xc_ps[:])
-            nc.vector.tensor_copy(out=rTf[:], in_=rt_ps[:])
-            nc.vector.tensor_tensor(out=r2T[:], in0=rTf[:], in1=rTf[:], op=ALU.mult)
-            nc.vector.tensor_scalar(out=rTm2[:], in0=rTf[:], scalar1=-2.0, scalar2=None, op0=ALU.mult)
+            nc.vector.tensor_scalar(out=rTm2[:], in0=rt_ps[:], scalar1=-2.0, scalar2=None, op0=ALU.mult)
+            nc.gpsimd.tensor_tensor(out=r2T[:], in0=rTm2[:], in1=rTm2[:], op=ALU.mult)
+
+        ec_bank = []
 
         def tables_2():
             ec_ps = bank([P, 4, P], F32)
             for t in range(4):
                 nc.tensor.matmul(out=ec_ps[:, t, :], lhsT=excT[:, t, :], rhs=r_sb[:], start=True, stop=True)
-            rr_ps = bank([P, P], F32)
-            nc.tensor.matmul(out=rr_ps[:], lhsT=ones_f[:], rhs=r2T[:], start=True, stop=True)
+            ec_bank.append(ec_ps)
+
+        def tables_3():
             nc.vector.tensor_copy(
-                out=ecg[:].rearrange("p (c t) -> p c t", t=4), in_=ec_ps[:].rearrange("p t c -> p c t")
+                out=ecg[:].rearrange("p (c t) -> p c t", t=4), in_=ec_bank[0][:].rearrange("p t c -> p c t")
             )
+            nc.vector.quantize_mx(out=ecr_c[:].bitcast(FP8X4), scales=ecr_s[:], in_=ecg[:])
+
+        def tables_4():
+            rr_ps = bank([P, P], F32)
+            nc.tensor.matmul(out=rr_ps[:], lhsT=quarter[:], rhs=r2T[:], start=True, stop=True)
             rrf = const.tile([P, P], F32, name="rrf")
             nc.vector.tensor_copy(out=rrf[:], in_=rr_ps[:])
             rr_h = const.tile([P, P], BF16, name="rr_h")
-            nc.vector.tensor_copy(out=rr_h[:], in_=rrf[:])
-            nc.vector.quantize_mx(out=ecr_c[:].bitcast(FP8X4), scales=ecr_s[:], in_=ecg[:])
+            nc.gpsimd.tensor_copy(out=rr_h[:], in_=rrf[:])
             rr_d = const.tile([P, P], F32, name="rr_d")
-            nc.vector.tensor_tensor(out=rr_d[:], in0=rrf[:], in1=rr_h[:], op=ALU.subtract)
+            nc.gpsimd.tensor_tensor(out=rr_d[:], in0=rrf[:], in1=rr_h[:], op=ALU.subtract)
             rr_m = const.tile([P, P], BF16, name="rr_m")
-            nc.vector.tensor_copy(out=rr_m[:], in_=rr_d[:])
-            nc.vector.memset(rr_w[:], 0.0)
-            nc.vector.tensor_copy(out=rr_w[0:32, :], in_=rr_h[0:32, :])
-            nc.vector.tensor_copy(out=rr_w[32:64, :], in_=rr_m[32:64, :])
-            nc.vector.tensor_tensor(
+            nc.gpsimd.tensor_copy(out=rr_m[:], in_=rr_d[:])
+            nc.gpsimd.memset(rr_w[:], 0.0)
+            nc.gpsimd.tensor_copy(out=rr_w[0:32, :], in_=rr_h[0:32, :])
+            nc.gpsimd.tensor_copy(out=rr_w[32:64, :], in_=rr_m[32:64, :])
+            nc.gpsimd.tensor_tensor(
                 out=rr_w[64:96, :], in0=rr_d[64:96, :], in1=rr_m[64:96, :], op=ALU.subtract
             )
 
@@ -345,8 +353,26 @@ def tile_minerva_detex_pb_t_kernel(tc, f_n, ex_n, ex_classes, class_reps, out):
         do_T(3)
         ex_Q(2)
         ex_Q(3)
+        do_T(4)
+        do_T(5)
         do_E(2, False)
         do_E(3, True)
+        do_E(4, False)
+        do_M(0)
+        do_M(1)
+        do_Q(1)
+        do_S(0)
+        do_V(0)
+        do_M(2)
+        do_M(3)
+        do_S(1)
+        do_V(1)
+        do_S(2)
+        do_QA(0)
+        do_V(2)
+        do_S(3)
+        do_V(3)
+        do_QA(1)
 
         def ok(m):
             return 0 <= m < N_MACRO
@@ -354,29 +380,30 @@ def tile_minerva_detex_pb_t_kernel(tc, f_n, ex_n, ex_classes, class_reps, out):
         def mid(m):
             return 0 <= m < LAST
 
-        do_M(0)
-        do_M(1)
-        do_S(0)
-        do_S(1)
-        do_V(0)
-        do_V(1)
         for m in range(N_MACRO + 2):
             y, z, a, b, c = m - 3, m - 2, m - 1, m, m + 1
+            if ok(m + PREFETCH):
+                load_f(2 * (m + PREFETCH))
+                load_f(2 * (m + PREFETCH) + 1)
             if ok(c):
-                for j in range(4):
+                for j in range(2 if m == 0 else 0, 4):
                     do_T(4 * c + j)
+            if m == 0:
+                tables_1()
+            if m == 1:
+                tables_2()
             if mid(z):
                 do_D_pe(z, 0, 4)
-            if ok(a):
+            if ok(a) and m > 1:
                 do_S(4 * a + 3)
-            if ok(c):
+            if ok(c) and m > 0:
                 do_E(4 * c, False)
-            if ok(a):
+            if ok(a) and m > 1:
                 do_V(4 * a + 2)
                 do_V(4 * a + 3)
-            if ok(b):
+            if ok(b) and m > 0:
                 do_Q(2 * b + 1)
-            if ok(a):
+            if ok(a) and m > 1:
                 do_QA(2 * a + 1)
             if ok(c):
                 do_E(4 * c + 1, False)
@@ -385,10 +412,12 @@ def tile_minerva_detex_pb_t_kernel(tc, f_n, ex_n, ex_classes, class_reps, out):
             if ok(b) and m > 0:
                 do_M(4 * b)
                 do_M(4 * b + 1)
-            if m == 0:
-                tables_1()
+            if m == 1:
+                tables_3()
             if mid(a):
                 do_C_pe(a, 0, 4)
+            if m == 1:
+                tables_4()
             if mid(z):
                 do_D_s(z, 0, 4)
             if ok(c):
@@ -399,18 +428,16 @@ def tile_minerva_detex_pb_t_kernel(tc, f_n, ex_n, ex_classes, class_reps, out):
                 do_S(4 * b)
                 do_V(4 * b)
                 do_S(4 * b + 1)
-            if ok(b):
+            if ok(b) and m > 0:
                 do_M(4 * b + 2)
                 do_M(4 * b + 3)
-            if m == 0:
-                tables_2()
             if ok(b) and m > 0:
                 do_V(4 * b + 1)
             if mid(a):
                 do_C_h(a, 0, 4)
                 do_C_v(a, 0, 4)
                 do_C_s(a, 0, 4)
-            if ok(b):
+            if ok(b) and m > 0:
                 do_QA(2 * b)
                 do_S(4 * b + 2)
             if a == LAST:

@@ -175,11 +175,7 @@ def tile_minerva_detex_pb_t_kernel(tc, f_n, ex_n, ex_classes, class_reps, out):
 
         def do_S(i):
             s2 = s2p.tile([P, 512], F32, name="s2", tag="s2")
-            nc.scalar.activation(
-                out=s2[:].rearrange("p (b t) -> p b t", t=4),
-                in_=sts[i][:].rearrange("p t b -> p b t"),
-                func=ACT.Square,
-            )
+            nc.scalar.activation(out=s2[:].rearrange("p (t b) -> p t b", t=4), in_=sts[i][:], func=ACT.Square)
             s2s[i] = s2
 
         def do_V(i):
@@ -187,9 +183,9 @@ def tile_minerva_detex_pb_t_kernel(tc, f_n, ex_n, ex_classes, class_reps, out):
             if half == 0:
                 ags[h] = agp.tile([P, 1024], BF16, name="ag", tag="ag", align_bytes=64)
             nc.vector.tensor_tensor(
-                out=ags[h][:, 512 * half : 512 * (half + 1)].rearrange("p (b t) -> p b t", t=4),
-                in0=sts[i][:].rearrange("p t b -> p b t"),
-                in1=s2s[i][:].rearrange("p (b t) -> p b t", t=4),
+                out=ags[h][:, 512 * half : 512 * (half + 1)].rearrange("p (c i t) -> p c t i", i=4, t=4),
+                in0=sts[i][:].rearrange("p t (c i) -> p c t i", i=4),
+                in1=s2s[i][:].rearrange("p (t c i) -> p c t i", t=4, i=4),
                 op=ALU.mult,
             )
 

@@ -15,40 +15,30 @@ P = 128
 B, D, F, C = 8192, 512, 1024, 128
 FLOPS = 2 * B * D * F + 2 * B * D * C + 2 * D * C * C + 3 * B * C * C
 
-MANUAL = True
-XT_BANKS = 2
-ST_BANKS = 4
-NEG_ON_GPSIMD = False
-E_V_EVEN = False
-E_V_ODD = True
-N_TILES = B // P
-N_PAIR = N_TILES // 2
 PREFETCH = 5
-N_MACRO = N_TILES // 4
+N_MACRO = B // (4 * P)
 LAST = N_MACRO - 1
+DIRECT = LAST - 1
 
 
 def tile_minerva_detex_pb_t_kernel(tc, f_n, ex_n, ex_classes, class_reps, out):
     nc = tc.nc
     with ExitStack() as ctx:
         const = ctx.enter_context(tc.tile_pool(name="const", bufs=1))
-        fpool = ctx.enter_context(tc.tile_pool(name="fpool", bufs=N_PAIR))
+        fpool = ctx.enter_context(tc.tile_pool(name="fpool", bufs=2 * (PREFETCH + 2)))
         fgp = ctx.enter_context(tc.tile_pool(name="fgp", bufs=4))
         fcp = ctx.enter_context(tc.tile_pool(name="fcp", bufs=5))
         s2p = ctx.enter_context(tc.tile_pool(name="s2p", bufs=4))
         agp = ctx.enter_context(tc.tile_pool(name="agp", bufs=3))
         acp = ctx.enter_context(tc.tile_pool(name="acp", bufs=3))
-        e3p = ctx.enter_context(tc.tile_pool(name="e3p", bufs=3))
-        psum = ctx.enter_context(tc.psum_pool(name="psum", bufs=1))
-        banks_used = []
+        e3p = ctx.enter_context(tc.tile_pool(name="e3p", bufs=4))
+        ps_x = ctx.enter_context(tc.psum_pool(name="ps_x", bufs=4))
+        ps_m = ctx.enter_context(tc.psum_pool(name="ps_m", bufs=3))
+        ps_e = ctx.enter_context(tc.psum_pool(name="ps_e", bufs=1))
+        ctx.enter_context(tc.manual_schedule())
 
-        def bank(shape, dtype):
-            n = len(banks_used)
-            banks_used.append(n)
-            return psum.tile(shape, dtype, name="bank%d" % (n % 8), tag="bank%d" % (n % 8))
-
-        if MANUAL:
-            ctx.enter_context(tc.manual_schedule())
+        def bank(pool, shape, dtype=F32):
+            return pool.tile(shape, dtype, name="bank", tag="bank")
 
         f_sbs = []
 
@@ -102,15 +92,15 @@ def tile_minerva_detex_pb_t_kernel(tc, f_n, ex_n, ex_classes, class_reps, out):
         acs = {}
         c3 = {}
 
-        def transposes(bank, words):
+        def transposes(xt, words):
             for g in range(2):
                 for u in range(2):
                     c0 = 256 * g + 128 * u
-                    nc.tensor.transpose(bank[:, g, u, :], words[:, c0 : c0 + P], ident[:])
+                    nc.tensor.transpose(xt[:, g, u, :], words[:, c0 : c0 + P], ident[:])
 
-        def copy_out(grouped, bank, on_vector):
-            dst = grouped.bitcast(F32).rearrange("p (g b u) -> p g b u", g=2, u=2)
-            src = bank[:].rearrange("p g u b -> p g b u")
+        def copy_out(words, xt, on_vector):
+            dst = words.bitcast(F32).rearrange("p (g b u) -> p g b u", g=2, u=2)
+            src = xt[:].rearrange("p g u b -> p g b u")
             if on_vector:
                 nc.vector.tensor_copy(out=dst, in_=src)
             else:
@@ -118,7 +108,7 @@ def tile_minerva_detex_pb_t_kernel(tc, f_n, ex_n, ex_classes, class_reps, out):
 
         def do_T(i):
             h, half = divmod(i, 2)
-            xt = bank([P, 2, 2, P], F32)
+            xt = bank(ps_x, [P, 2, 2, P])
             transposes(xt, f_sbs[h][:].bitcast(F32)[:, 512 * half : 512 * (half + 1)])
             xts[i] = xt
 
@@ -139,7 +129,7 @@ def tile_minerva_detex_pb_t_kernel(tc, f_n, ex_n, ex_classes, class_reps, out):
         ex_cs = []
 
         def ex_T(t):
-            xe = bank([P, 2, 2, P], F32)
+            xe = bank(ps_m if t < 3 else ps_e, [P, 2, 2, P])
             transposes(xe, ex_sbs[t][:].bitcast(F32))
             ex_banks.append(xe)
 
@@ -157,7 +147,7 @@ def tile_minerva_detex_pb_t_kernel(tc, f_n, ex_n, ex_classes, class_reps, out):
         def do_M(i):
             h, half = divmod(i, 2)
             fc, fs = fcs[h]
-            st = bank([P, 4, P], F32)
+            st = bank(ps_m, [P, 4, P])
             for t in range(4):
                 ex_c, ex_s = ex_cs[t]
                 for g in range(2):
@@ -179,28 +169,23 @@ def tile_minerva_detex_pb_t_kernel(tc, f_n, ex_n, ex_classes, class_reps, out):
             s2s[i] = s2
 
         def do_V(i):
-            h, half = divmod(i, 2)
-            if half == 0:
-                ags[h] = agp.tile([P, 1024], BF16, name="ag", tag="ag", align_bytes=64)
+            m, j = divmod(i, 4)
+            if j == 0:
+                ags[m] = agp.tile([P, 2048], BF16, name="ag", tag="ag", align_bytes=64)
             nc.vector.tensor_tensor(
-                out=ags[h][:, 512 * half : 512 * (half + 1)].rearrange("p (c i t) -> p c t i", i=4, t=4),
+                out=ags[m][:, 512 * j : 512 * (j + 1)].rearrange("p (c i t) -> p c t i", i=4, t=4),
                 in0=sts[i][:].rearrange("p t (c i) -> p c t i", i=4),
                 in1=s2s[i][:].rearrange("p (t c i) -> p c t i", t=4, i=4),
                 op=ALU.mult,
             )
 
-        def do_QA(h):
-            m, pair = divmod(h, 2)
-            if pair == 0 or m == LAST:
-                ac = acp.tile([P, 512], U32, name="ac", tag="ac", align_bytes=64)
-                asc = acp.tile([P, 512], U8, name="asc", tag="asc", align_bytes=64)
-                acs[(m, pair)] = (ac, asc)
-            ac, asc = acs[(m, pair if m == LAST else 0)]
+        def do_QA(m, j0, nj):
+            ac = acp.tile([P, nj * P], U32, name="ac", tag="ac%d" % j0, align_bytes=64)
+            asc = acp.tile([P, nj * P], U8, name="asc", tag="asc%d" % j0, align_bytes=64)
             nc.vector.quantize_mx(
-                out=ac[:, 256 * pair : 256 * (pair + 1)].bitcast(FP8X4),
-                scales=asc[:, 256 * pair : 256 * (pair + 1)],
-                in_=ags[h][:],
+                out=ac[:].bitcast(FP8X4), scales=asc[:], in_=ags[m][:, 512 * j0 : 512 * (j0 + nj)]
             )
+            acs[(m, j0)] = (ac, asc)
 
         excT = const.tile([P, 4, P], BF16, name="excT")
         ecg = const.tile([P, 512], BF16, name="ecg", align_bytes=64)
@@ -209,34 +194,41 @@ def tile_minerva_detex_pb_t_kernel(tc, f_n, ex_n, ex_classes, class_reps, out):
         rTm2 = const.tile([P, P], BF16, name="rTm2")
         r2T = const.tile([P, P], F32, name="r2T")
         rr_w = const.tile([P, P], BF16, name="rr_w")
+        t_bank = []
+        ec_bank = []
 
         def tables_1():
-            xc_ps = bank([P, 4, P], BF16)
+            xc_ps = bank(ps_x, [P, 4, P], BF16)
             for t in range(4):
                 nc.tensor.transpose(xc_ps[:, t, :], exc_sb[:, t * P : (t + 1) * P], ident_b[:])
-            rt_ps = bank([P, P], BF16)
+            rt_ps = bank(ps_x, [P, P], BF16)
             nc.tensor.transpose(rt_ps[:], r_sb[:], ident_b[:])
+            t_bank.extend([xc_ps, rt_ps])
+
+        def tables_1v():
+            xc_ps, rt_ps = t_bank
             nc.vector.tensor_copy(out=excT[:], in_=xc_ps[:])
             nc.vector.tensor_scalar(out=rTm2[:], in0=rt_ps[:], scalar1=-2.0, scalar2=None, op0=ALU.mult)
             nc.gpsimd.tensor_tensor(out=r2T[:], in0=rTm2[:], in1=rTm2[:], op=ALU.mult)
 
-        ec_bank = []
-
         def tables_2():
-            ec_ps = bank([P, 4, P], F32)
+            ec_ps = bank(ps_e, [P, 4, P])
             for t in range(4):
                 nc.tensor.matmul(out=ec_ps[:, t, :], lhsT=excT[:, t, :], rhs=r_sb[:], start=True, stop=True)
-            ec_bank.append(ec_ps)
+            rr_ps = bank(ps_x, [P, P])
+            nc.tensor.matmul(out=rr_ps[:], lhsT=quarter[:], rhs=r2T[:], start=True, stop=True)
+            ec_bank.extend([ec_ps, rr_ps])
 
         def tables_3():
             nc.vector.tensor_copy(
                 out=ecg[:].rearrange("p (c t) -> p c t", t=4), in_=ec_bank[0][:].rearrange("p t c -> p c t")
             )
-            nc.vector.quantize_mx(out=ecr_c[:].bitcast(FP8X4), scales=ecr_s[:], in_=ecg[:])
 
         def tables_4():
-            rr_ps = bank([P, P], F32)
-            nc.tensor.matmul(out=rr_ps[:], lhsT=quarter[:], rhs=r2T[:], start=True, stop=True)
+            nc.vector.quantize_mx(out=ecr_c[:].bitcast(FP8X4), scales=ecr_s[:], in_=ecg[:])
+
+        def tables_5():
+            rr_ps = ec_bank[1]
             rrf = const.tile([P, P], F32, name="rrf")
             nc.vector.tensor_copy(out=rrf[:], in_=rr_ps[:])
             rr_h = const.tile([P, P], BF16, name="rr_h")
@@ -253,21 +245,20 @@ def tile_minerva_detex_pb_t_kernel(tc, f_n, ex_n, ex_classes, class_reps, out):
             )
 
         def do_C_pe(m, j0, nj):
-            ac, asc = acs[(m, j0 // 2)]
-            cols = slice(j0 * P, (j0 + nj) * P)
-            eT = bank([P, nj * P], F32)
+            ac, asc = acs[(m, j0)]
+            eT = bank(ps_e if nj == 4 else ps_x, [P, nj * P])
             nc.tensor.matmul_mx(
                 out=eT[:],
                 lhsT=ecr_c[:].bitcast(FP8X4),
                 lhsT_scale=ecr_s[:],
-                rhs=ac[:, cols].bitcast(FP8X4),
-                rhs_scale=asc[:, cols],
+                rhs=ac[:].bitcast(FP8X4),
+                rhs_scale=asc[:],
                 start=True,
                 stop=True,
             )
-            eb = bank([P, nj, P], F32)
+            eb = bank(ps_x, [P, nj, P])
             for j in range(nj):
-                jc = slice((j0 + j) * P, (j0 + j + 1) * P)
+                jc = slice(j * P, (j + 1) * P)
                 nc.tensor.matmul_mx(
                     out=eb[:, j, :],
                     lhsT=ac[:, jc].bitcast(FP8X4),
@@ -279,15 +270,25 @@ def tile_minerva_detex_pb_t_kernel(tc, f_n, ex_n, ex_classes, class_reps, out):
                 )
             c3[(m, j0)] = {"eT": eT, "eb": eb}
 
-        def do_C_v(m, j0, nj):
-            em = e3p.tile([P, nj * P], BF16, name="em", tag="em")
-            nc.vector.tensor_tensor(out=em[:], in0=c3[(m, j0)]["eT"][:], in1=c3[(m, j0)]["eh"][:], op=ALU.subtract)
-            c3[(m, j0)]["em"] = em
-
         def do_C_h(m, j0, nj):
-            eh = e3p.tile([P, nj * P], BF16, name="eh", tag="eh")
-            nc.scalar.copy(out=eh[:], in_=c3[(m, j0)]["eT"][:])
-            c3[(m, j0)]["eh"] = eh
+            t = c3[(m, j0)]
+            t["eh"] = e3p.tile([P, nj * P], BF16, name="eh", tag="eh")
+            t["em"] = e3p.tile([P, nj * P], BF16, name="em", tag="em")
+            if m >= DIRECT:
+                nc.scalar.copy(out=t["eh"][:], in_=t["eT"][:])
+            else:
+                t["eTs"] = e3p.tile([P, nj * P], F32, name="eTs", tag="eTs")
+                nc.scalar.copy(out=t["eTs"][:], in_=t["eT"][:])
+
+        def do_C_m(m, j0, nj):
+            t = c3[(m, j0)]
+            if m >= DIRECT:
+                nc.vector.tensor_tensor(out=t["em"][:], in0=t["eT"][:], in1=t["eh"][:], op=ALU.subtract)
+            else:
+                nc.gpsimd.tensor_scalar(
+                    out=t["eh"][:], in0=t["eTs"][:], scalar1=1.0, scalar2=0.0, op0=ALU.mult, op1=ALU.add
+                )
+                nc.gpsimd.tensor_tensor(out=t["em"][:], in0=t["eTs"][:], in1=t["eh"][:], op=ALU.subtract)
 
         def do_C_s(m, j0, nj):
             ee = e3p.tile([P, nj], F32, name="ee", tag="ee")
@@ -299,7 +300,7 @@ def tile_minerva_detex_pb_t_kernel(tc, f_n, ex_n, ex_classes, class_reps, out):
             c3[(m, j0)]["ee"] = ee
 
         def do_D_pe(m, j0, nj):
-            db = bank([P, nj, P], F32)
+            db = bank(ps_x, [P, nj, P])
             eh, em = c3[(m, j0)]["eh"], c3[(m, j0)]["em"]
             for j in range(nj):
                 jc = slice(j * P, (j + 1) * P)
@@ -322,9 +323,9 @@ def tile_minerva_detex_pb_t_kernel(tc, f_n, ex_n, ex_classes, class_reps, out):
 
         def do_D_v(m, j0, nj):
             o = e3p.tile([P, nj * P], F32, name="o", tag="o")
-            eng = nc.gpsimd if NEG_ON_GPSIMD else nc.vector
+            eng = nc.vector if m >= DIRECT else nc.gpsimd
             eng.tensor_scalar(
-                out=o[:], in0=c3[(m, j0)]["sq"][:], scalar1=-1.0, scalar2=0.0, op0=ALU.mult, op1=ALU.min
+                out=o[:], in0=c3[(m, j0)]["sq"][:], scalar1=-1.0, scalar2=0.0, op0=ALU.mult, op1=ALU.add
             )
             r0 = 512 * m + P * j0
             nc.sync.dma_start(
@@ -349,105 +350,105 @@ def tile_minerva_detex_pb_t_kernel(tc, f_n, ex_n, ex_classes, class_reps, out):
         do_T(3)
         ex_Q(2)
         ex_Q(3)
-        do_T(4)
-        do_T(5)
         do_E(2, False)
         do_E(3, True)
-        do_E(4, False)
         do_M(0)
         do_M(1)
         do_Q(1)
         do_S(0)
-        do_V(0)
-        do_M(2)
-        do_M(3)
-        do_S(1)
-        do_V(1)
-        do_S(2)
-        do_QA(0)
-        do_V(2)
-        do_S(3)
-        do_V(3)
-        do_QA(1)
 
         def ok(m):
             return 0 <= m < N_MACRO
 
-        def mid(m):
-            return 0 <= m < LAST
-
-        for m in range(N_MACRO + 2):
+        for m in range(N_MACRO):
             y, z, a, b, c = m - 3, m - 2, m - 1, m, m + 1
             if ok(m + PREFETCH):
                 load_f(2 * (m + PREFETCH))
                 load_f(2 * (m + PREFETCH) + 1)
+            if m == 0:
+                do_M(2)
+                do_M(3)
             if ok(c):
-                for j in range(2 if m == 0 else 0, 4):
+                for j in (0, 2, 1, 3):
                     do_T(4 * c + j)
             if m == 0:
                 tables_1()
             if m == 1:
                 tables_2()
-            if mid(z):
-                do_D_pe(z, 0, 4)
-            if ok(a) and m > 1:
-                do_S(4 * a + 3)
-            if ok(c) and m > 0:
-                do_E(4 * c, False)
-            if ok(a) and m > 1:
-                do_V(4 * a + 2)
-                do_V(4 * a + 3)
-            if ok(b) and m > 0:
-                do_Q(2 * b + 1)
-            if ok(a) and m > 1:
-                do_QA(2 * a + 1)
-            if ok(c):
-                do_E(4 * c + 1, False)
-                do_E(4 * c + 3, True)
-                do_E(4 * c + 2, False)
-            if ok(b) and m > 0:
-                do_M(4 * b)
-                do_M(4 * b + 1)
+            if ok(z):
+                do_C_m(z, 0, 4)
+            if ok(y):
+                do_D_v(y, 0, 4)
+            do_V(4 * b)
+            do_S(4 * b + 1)
+            do_V(4 * b + 1)
             if m == 1:
                 tables_3()
-            if mid(a):
-                do_C_pe(a, 0, 4)
+            if m == 0:
+                do_S(2)
+                do_S(3)
+                do_V(2)
+                do_V(3)
+                do_QA(0, 0, 4)
+            if ok(c):
+                do_E(4 * c, False)
+                do_E(4 * c + 2, m > 0)
+                do_E(4 * c + 1, False)
+                do_E(4 * c + 3, m > 0)
             if m == 1:
                 tables_4()
-            if mid(z):
-                do_D_s(z, 0, 4)
+                tables_5()
             if ok(c):
                 do_Q(2 * c)
-            if mid(z):
-                do_D_v(z, 0, 4)
-            if ok(b) and m > 0:
-                do_S(4 * b)
-                do_V(4 * b)
-                do_S(4 * b + 1)
-            if ok(b) and m > 0:
+            if m == 0:
+                tables_1v()
+            if m > 0:
                 do_M(4 * b + 2)
                 do_M(4 * b + 3)
-            if ok(b) and m > 0:
-                do_V(4 * b + 1)
-            if mid(a):
-                do_C_h(a, 0, 4)
-                do_C_v(a, 0, 4)
-                do_C_s(a, 0, 4)
-            if ok(b) and m > 0:
-                do_QA(2 * b)
+            if m > 0:
                 do_S(4 * b + 2)
-            if a == LAST:
-                do_C_pe(LAST, 0, 2)
-                do_C_h(LAST, 0, 2)
-                do_C_v(LAST, 0, 2)
-                do_C_s(LAST, 0, 2)
-                do_C_pe(LAST, 2, 2)
-                do_C_h(LAST, 2, 2)
-                do_D_pe(LAST, 0, 2)
-                do_C_v(LAST, 2, 2)
-                do_C_s(LAST, 2, 2)
-                do_D_s(LAST, 0, 2)
-                do_D_pe(LAST, 2, 2)
-                do_D_v(LAST, 0, 2)
-                do_D_s(LAST, 2, 2)
-                do_D_v(LAST, 2, 2)
+                do_S(4 * b + 3)
+                if b == LAST:
+                    do_QA(b, 0, 2)
+                do_V(4 * b + 2)
+                do_V(4 * b + 3)
+            if ok(a):
+                do_C_pe(a, 0, 4)
+            if ok(z):
+                do_D_pe(z, 0, 4)
+            if ok(c):
+                do_Q(2 * c + 1)
+                if m > 0:
+                    do_QA(b, 0, 4)
+                do_M(4 * c)
+                do_M(4 * c + 1)
+            else:
+                do_QA(b, 2, 2)
+                do_C_pe(b, 0, 2)
+            if ok(a):
+                do_C_s(a, 0, 4)
+            if ok(z):
+                do_D_s(z, 0, 4)
+            if ok(a):
+                do_C_h(a, 0, 4)
+            if ok(c):
+                do_S(4 * c)
+
+        do_C_m(LAST - 1, 0, 4)
+        do_D_v(LAST - 2, 0, 4)
+        do_C_h(LAST, 0, 2)
+        do_C_m(LAST, 0, 2)
+        do_C_s(LAST, 0, 2)
+        do_D_pe(LAST - 1, 0, 4)
+        do_C_pe(LAST, 2, 2)
+        do_D_s(LAST - 1, 0, 4)
+        do_D_v(LAST - 1, 0, 4)
+        do_C_h(LAST, 2, 2)
+        do_C_m(LAST, 2, 2)
+        do_C_s(LAST, 2, 2)
+        do_D_pe(LAST, 0, 2)
+        do_D_s(LAST, 0, 2)
+        do_D_pe(LAST, 2, 2)
+        do_D_v(LAST, 0, 2)
+        do_D_s(LAST, 2, 2)
+        do_D_v(LAST, 2, 2)

@@ -18,7 +18,6 @@ FLOPS = 2 * B * D * F + 2 * B * D * C + 2 * D * C * C + 3 * B * C * C
 PREFETCH = 5
 N_MACRO = B // (4 * P)
 LAST = N_MACRO - 1
-DIRECT = LAST - 1
 
 
 def tile_minerva_detex_pb_t_kernel(tc, f_n, ex_n, ex_classes, class_reps, out):
@@ -50,13 +49,22 @@ def tile_minerva_detex_pb_t_kernel(tc, f_n, ex_n, ex_classes, class_reps, out):
             )
             f_sbs.append(f_sb)
 
-        load_f(0)
+        f_0 = fpool.tile([P, 2 * F], BF16, name="f_sb", tag="f_sb")
+        f_sbs.append(f_0)
+
+        def load_f0(i):
+            nc.sync.dma_start(
+                out=f_0[:, i * F : (i + 1) * F], in_=f_n[0:256, :].rearrange("(p i) k -> p i k", i=2)[:, i, :]
+            )
+
+        load_f0(0)
         ex_rows = ex_n.rearrange("(p t) k -> p t k", t=4)
         ex_sbs = []
         for t in range(4):
             ex_sb = const.tile([P, F], BF16, name="ex_sb%d" % t)
             nc.sync.dma_start(out=ex_sb[:], in_=ex_rows[:, t, :])
             ex_sbs.append(ex_sb)
+        load_f0(1)
         load_f(1)
         load_f(2)
         load_f(3)
@@ -67,7 +75,7 @@ def tile_minerva_detex_pb_t_kernel(tc, f_n, ex_n, ex_classes, class_reps, out):
         )
         r_sb = const.tile([P, C], BF16, name="r_sb")
         nc.sync.dma_start(out=r_sb[:], in_=class_reps)
-        for h in range(4, 2 * PREFETCH):
+        for h in range(4, 2 * PREFETCH + 2):
             load_f(h)
 
         ident = const.tile([P, P], F32, name="ident")
@@ -98,9 +106,9 @@ def tile_minerva_detex_pb_t_kernel(tc, f_n, ex_n, ex_classes, class_reps, out):
                     c0 = 256 * g + 128 * u
                     nc.tensor.transpose(xt[:, g, u, :], words[:, c0 : c0 + P], ident[:])
 
-        def copy_out(words, xt, on_vector):
-            dst = words.bitcast(F32).rearrange("p (g b u) -> p g b u", g=2, u=2)
-            src = xt[:].rearrange("p g u b -> p g b u")
+        def copy_out(words, xt, on_vector, g0=0, g1=2):
+            dst = words.bitcast(F32).rearrange("p (g b u) -> p g b u", g=2, u=2)[:, g0:g1]
+            src = xt[:].rearrange("p g u b -> p g b u")[:, g0:g1]
             if on_vector:
                 nc.vector.tensor_copy(out=dst, in_=src)
             else:
@@ -112,17 +120,28 @@ def tile_minerva_detex_pb_t_kernel(tc, f_n, ex_n, ex_classes, class_reps, out):
             transposes(xt, f_sbs[h][:].bitcast(F32)[:, 512 * half : 512 * (half + 1)])
             xts[i] = xt
 
-        def do_E(i, on_vector):
+        def do_E(i, on_vector, g0=0, g1=2):
             h, half = divmod(i, 2)
             if h not in fgs:
                 fgs[h] = fgp.tile([P, 2048], BF16, name="fg", tag="fg", align_bytes=64)
-            copy_out(fgs[h][:, 1024 * half : 1024 * (half + 1)], xts[i], on_vector)
+            copy_out(fgs[h][:, 1024 * half : 1024 * (half + 1)], xts[i], on_vector, g0, g1)
 
         def do_Q(h):
             fc = fcp.tile([P, 512], U32, name="fc", tag="fc", align_bytes=64)
             fs = fcp.tile([P, 512], U8, name="fs", tag="fs", align_bytes=64)
             nc.vector.quantize_mx(out=fc[:].bitcast(FP8X4), scales=fs[:], in_=fgs[h][:])
             fcs[h] = (fc, fs)
+
+        def do_Q0(half):
+            if half == 0:
+                fc = fcp.tile([P, 512], U32, name="fc", tag="fc", align_bytes=64)
+                fs = fcp.tile([P, 512], U8, name="fs", tag="fs", align_bytes=64)
+                fcs[0] = (fc, fs)
+            fc, fs = fcs[0]
+            cols = slice(256 * half, 256 * (half + 1))
+            nc.vector.quantize_mx(
+                out=fc[:, cols].bitcast(FP8X4), scales=fs[:, cols], in_=fgs[0][:, 1024 * half : 1024 * (half + 1)]
+            )
 
         ex_banks = []
         ex_gs = []
@@ -274,21 +293,11 @@ def tile_minerva_detex_pb_t_kernel(tc, f_n, ex_n, ex_classes, class_reps, out):
             t = c3[(m, j0)]
             t["eh"] = e3p.tile([P, nj * P], BF16, name="eh", tag="eh")
             t["em"] = e3p.tile([P, nj * P], BF16, name="em", tag="em")
-            if m >= DIRECT:
-                nc.scalar.copy(out=t["eh"][:], in_=t["eT"][:])
-            else:
-                t["eTs"] = e3p.tile([P, nj * P], F32, name="eTs", tag="eTs")
-                nc.scalar.copy(out=t["eTs"][:], in_=t["eT"][:])
+            nc.scalar.copy(out=t["eh"][:], in_=t["eT"][:])
 
         def do_C_m(m, j0, nj):
             t = c3[(m, j0)]
-            if m >= DIRECT:
-                nc.vector.tensor_tensor(out=t["em"][:], in0=t["eT"][:], in1=t["eh"][:], op=ALU.subtract)
-            else:
-                nc.gpsimd.tensor_scalar(
-                    out=t["eh"][:], in0=t["eTs"][:], scalar1=1.0, scalar2=0.0, op0=ALU.mult, op1=ALU.add
-                )
-                nc.gpsimd.tensor_tensor(out=t["em"][:], in0=t["eTs"][:], in1=t["eh"][:], op=ALU.subtract)
+            nc.vector.tensor_tensor(out=t["em"][:], in0=t["eT"][:], in1=t["eh"][:], op=ALU.subtract)
 
         def do_C_s(m, j0, nj):
             ee = e3p.tile([P, nj], F32, name="ee", tag="ee")
@@ -323,7 +332,7 @@ def tile_minerva_detex_pb_t_kernel(tc, f_n, ex_n, ex_classes, class_reps, out):
 
         def do_D_v(m, j0, nj):
             o = e3p.tile([P, nj * P], F32, name="o", tag="o")
-            eng = nc.vector if m >= DIRECT else nc.gpsimd
+            eng = nc.vector if m >= LAST - 1 else nc.gpsimd
             eng.tensor_scalar(
                 out=o[:], in0=c3[(m, j0)]["sq"][:], scalar1=-1.0, scalar2=0.0, op0=ALU.mult, op1=ALU.add
             )
@@ -334,92 +343,104 @@ def tile_minerva_detex_pb_t_kernel(tc, f_n, ex_n, ex_classes, class_reps, out):
             )
 
         do_T(0)
-        do_T(1)
         do_E(0, False)
-        do_E(1, True)
         for t in range(4):
             ex_T(t)
-        ex_E(0, False)
-        ex_E(1, True)
-        do_Q(0)
+        ex_E(0, True)
+        ex_E(1, False)
+        do_Q0(0)
         ex_Q(0)
-        ex_E(2, False)
-        ex_E(3, True)
+        ex_E(2, True)
+        ex_E(3, False)
         ex_Q(1)
-        do_T(2)
-        do_T(3)
+        do_T(1)
         ex_Q(2)
         ex_Q(3)
+        do_M(0)
+        do_E(1, True)
+        do_T(2)
+        do_T(3)
+        do_S(0)
+        do_Q0(1)
         do_E(2, False)
         do_E(3, True)
-        do_M(0)
         do_M(1)
+        do_T(4)
+        do_T(5)
         do_Q(1)
-        do_S(0)
+        do_S(1)
+        do_V(0)
+        do_E(4, False)
+        do_E(5, True)
+        do_M(2)
+        do_M(3)
+        do_V(1)
+        do_Q(2)
+        do_T(6)
+        do_T(7)
+        do_S(2)
+        do_E(6, False)
+        do_S(3)
+        do_E(7, False)
+        do_M(4)
+        do_M(5)
+        do_V(2)
+        do_V(3)
+        tables_1()
+        do_QA(0, 0, 4)
+        do_Q(3)
+        tables_1v()
+        do_S(4)
 
         def ok(m):
             return 0 <= m < N_MACRO
 
-        for m in range(N_MACRO):
+        for m in range(1, N_MACRO):
             y, z, a, b, c = m - 3, m - 2, m - 1, m, m + 1
             if ok(m + PREFETCH):
                 load_f(2 * (m + PREFETCH))
                 load_f(2 * (m + PREFETCH) + 1)
-            if m == 0:
-                do_M(2)
-                do_M(3)
             if ok(c):
                 for j in (0, 2, 1, 3):
                     do_T(4 * c + j)
-            if m == 0:
-                tables_1()
             if m == 1:
                 tables_2()
             if ok(z):
                 do_C_m(z, 0, 4)
             if ok(y):
+                do_D_s(y, 0, 4)
                 do_D_v(y, 0, 4)
             do_V(4 * b)
             do_S(4 * b + 1)
             do_V(4 * b + 1)
             if m == 1:
                 tables_3()
-            if m == 0:
-                do_S(2)
-                do_S(3)
-                do_V(2)
-                do_V(3)
-                do_QA(0, 0, 4)
             if ok(c):
                 do_E(4 * c, False)
-                do_E(4 * c + 2, m > 0)
+                do_E(4 * c + 2, True)
                 do_E(4 * c + 1, False)
-                do_E(4 * c + 3, m > 0)
+                do_E(4 * c + 3, False, 0, 1)
+                do_E(4 * c + 3, True, 1, 2)
             if m == 1:
                 tables_4()
                 tables_5()
             if ok(c):
                 do_Q(2 * c)
-            if m == 0:
-                tables_1v()
-            if m > 0:
-                do_M(4 * b + 2)
-                do_M(4 * b + 3)
-            if m > 0:
-                do_S(4 * b + 2)
-                do_S(4 * b + 3)
-                if b == LAST:
-                    do_QA(b, 0, 2)
-                do_V(4 * b + 2)
-                do_V(4 * b + 3)
+            do_M(4 * b + 2)
+            do_M(4 * b + 3)
+            do_S(4 * b + 2)
+            do_S(4 * b + 3)
+            if b == LAST:
+                do_QA(b, 0, 2)
+            do_V(4 * b + 2)
+            do_V(4 * b + 3)
             if ok(a):
                 do_C_pe(a, 0, 4)
             if ok(z):
                 do_D_pe(z, 0, 4)
             if ok(c):
                 do_Q(2 * c + 1)
-                if m > 0:
-                    do_QA(b, 0, 4)
+                do_QA(b, 0, 4)
                 do_M(4 * c)
                 do_M(4 * c + 1)
             else:
@@ -427,14 +448,13 @@ def tile_minerva_detex_pb_t_kernel(tc, f_n, ex_n, ex_classes, class_reps, out):
                 do_C_pe(b, 0, 2)
             if ok(a):
                 do_C_s(a, 0, 4)
-            if ok(z):
-                do_D_s(z, 0, 4)
             if ok(a):
                 do_C_h(a, 0, 4)
             if ok(c):
                 do_S(4 * c)
 
         do_C_m(LAST - 1, 0, 4)
+        do_D_s(LAST - 2, 0, 4)
         do_D_v(LAST - 2, 0, 4)
         do_C_h(LAST, 0, 2)
         do_C_m(LAST, 0, 2)

@@ -18,6 +18,7 @@ FLOPS = 2 * B * D * F + 2 * B * D * C + 2 * D * C * C + 3 * B * C * C
 PREFETCH = 5
 N_MACRO = B // (4 * P)
 LAST = N_MACRO - 1
+E_SPLIT = 80
 
 
 def tile_minerva_detex_pb_t_kernel(tc, f_n, ex_n, ex_classes, class_reps, out):
@@ -106,9 +107,9 @@ def tile_minerva_detex_pb_t_kernel(tc, f_n, ex_n, ex_classes, class_reps, out):
                     c0 = 256 * g + 128 * u
                     nc.tensor.transpose(xt[:, g, u, :], words[:, c0 : c0 + P], ident[:])
 
-        def copy_out(words, xt, on_vector, g0=0, g1=2):
-            dst = words.bitcast(F32).rearrange("p (g b u) -> p g b u", g=2, u=2)[:, g0:g1]
-            src = xt[:].rearrange("p g u b -> p g b u")[:, g0:g1]
+        def copy_out(words, xt, on_vector, b0=0, b1=P):
+            dst = words.bitcast(F32).rearrange("p (g b u) -> p g b u", g=2, u=2)[:, :, b0:b1, :]
+            src = xt[:].rearrange("p g u b -> p g b u")[:, :, b0:b1, :]
             if on_vector:
                 nc.vector.tensor_copy(out=dst, in_=src)
             else:
@@ -120,11 +121,11 @@ def tile_minerva_detex_pb_t_kernel(tc, f_n, ex_n, ex_classes, class_reps, out):
             transposes(xt, f_sbs[h][:].bitcast(F32)[:, 512 * half : 512 * (half + 1)])
             xts[i] = xt
 
-        def do_E(i, on_vector, g0=0, g1=2):
+        def do_E(i, on_vector, b0=0, b1=P):
             h, half = divmod(i, 2)
             if h not in fgs:
                 fgs[h] = fgp.tile([P, 2048], BF16, name="fg", tag="fg", align_bytes=64)
-            copy_out(fgs[h][:, 1024 * half : 1024 * (half + 1)], xts[i], on_vector, g0, g1)
+            copy_out(fgs[h][:, 1024 * half : 1024 * (half + 1)], xts[i], on_vector, b0, b1)
 
         def do_Q(h):
             fc = fcp.tile([P, 512], U32, name="fc", tag="fc", align_bytes=64)
@@ -226,7 +227,7 @@ def tile_minerva_detex_pb_t_kernel(tc, f_n, ex_n, ex_classes, class_reps, out):
 
         def tables_1v():
             xc_ps, rt_ps = t_bank
-            nc.vector.tensor_copy(out=excT[:], in_=xc_ps[:])
+            nc.scalar.copy(out=excT[:], in_=xc_ps[:])
             nc.vector.tensor_scalar(out=rTm2[:], in0=rt_ps[:], scalar1=-2.0, scalar2=None, op0=ALU.mult)
             nc.gpsimd.tensor_tensor(out=r2T[:], in0=rTm2[:], in1=rTm2[:], op=ALU.mult)
 
@@ -249,7 +250,7 @@ def tile_minerva_detex_pb_t_kernel(tc, f_n, ex_n, ex_classes, class_reps, out):
         def tables_5():
             rr_ps = ec_bank[1]
             rrf = const.tile([P, P], F32, name="rrf")
-            nc.vector.tensor_copy(out=rrf[:], in_=rr_ps[:])
+            nc.scalar.copy(out=rrf[:], in_=rr_ps[:])
             rr_h = const.tile([P, P], BF16, name="rr_h")
             nc.gpsimd.tensor_copy(out=rr_h[:], in_=rrf[:])
             rr_d = const.tile([P, P], F32, name="rr_d")
@@ -289,11 +290,14 @@ def tile_minerva_detex_pb_t_kernel(tc, f_n, ex_n, ex_classes, class_reps, out):
                 )
             c3[(m, j0)] = {"eT": eT, "eb": eb}
 
-        def do_C_h(m, j0, nj):
+        def do_C_h(m, j0, nj, on_vector=False):
             t = c3[(m, j0)]
             t["eh"] = e3p.tile([P, nj * P], BF16, name="eh", tag="eh")
             t["em"] = e3p.tile([P, nj * P], BF16, name="em", tag="em")
-            nc.scalar.copy(out=t["eh"][:], in_=t["eT"][:])
+            if on_vector:
+                nc.vector.tensor_copy(out=t["eh"][:], in_=t["eT"][:])
+            else:
+                nc.scalar.copy(out=t["eh"][:], in_=t["eT"][:])
 
         def do_C_m(m, j0, nj):
             t = c3[(m, j0)]
@@ -395,14 +399,13 @@ def tile_minerva_detex_pb_t_kernel(tc, f_n, ex_n, ex_classes, class_reps, out):
         def ok(m):
             return 0 <= m < N_MACRO
 
-        for m in range(1, N_MACRO):
+        for m in range(1, LAST):
             y, z, a, b, c = m - 3, m - 2, m - 1, m, m + 1
             if ok(m + PREFETCH):
                 load_f(2 * (m + PREFETCH))
                 load_f(2 * (m + PREFETCH) + 1)
-            if ok(c):
-                for j in (0, 2, 1, 3):
-                    do_T(4 * c + j)
+            for j in (1, 0, 2, 3):
+                do_T(4 * c + j)
             if m == 1:
                 tables_2()
             if ok(z):
@@ -411,64 +414,71 @@ def tile_minerva_detex_pb_t_kernel(tc, f_n, ex_n, ex_classes, class_reps, out):
                 do_D_s(y, 0, 4)
                 do_D_v(y, 0, 4)
             do_V(4 * b)
+            do_E(4 * c + 1, False, E_SPLIT, P)
             do_S(4 * b + 1)
-            do_V(4 * b + 1)
             if m == 1:
                 tables_3()
-            if ok(c):
-                do_E(4 * c, False)
-                do_E(4 * c + 2, True)
-                do_E(4 * c + 1, False)
-                do_E(4 * c + 3, False, 0, 1)
-                do_E(4 * c + 3, True, 1, 2)
+            do_E(4 * c + 1, True, 0, E_SPLIT)
+            do_E(4 * c, True)
+            do_V(4 * b + 1)
+            do_E(4 * c + 2, False)
+            do_E(4 * c + 3, False)
             if m == 1:
                 tables_4()
                 tables_5()
-            if ok(c):
-                do_Q(2 * c)
+            do_Q(2 * c)
             do_M(4 * b + 2)
             do_M(4 * b + 3)
             do_S(4 * b + 2)
             do_S(4 * b + 3)
-            if b == LAST:
-                do_QA(b, 0, 2)
             do_V(4 * b + 2)
             do_V(4 * b + 3)
-            if ok(a):
-                do_C_pe(a, 0, 4)
+            do_C_pe(a, 0, 4)
             if ok(z):
                 do_D_pe(z, 0, 4)
-            if ok(c):
-                do_Q(2 * c + 1)
-                do_QA(b, 0, 4)
-                do_M(4 * c)
-                do_M(4 * c + 1)
-            else:
-                do_QA(b, 2, 2)
-                do_C_pe(b, 0, 2)
-            if ok(a):
-                do_C_s(a, 0, 4)
-            if ok(a):
-                do_C_h(a, 0, 4)
-            if ok(c):
-                do_S(4 * c)
+            do_Q(2 * c + 1)
+            do_QA(b, 0, 4)
+            do_M(4 * c)
+            do_M(4 * c + 1)
+            do_C_s(a, 0, 4)
+            do_C_h(a, 0, 4)
+            do_S(4 * c)
 
+        do_C_m(LAST - 2, 0, 4)
+        do_D_s(LAST - 3, 0, 4)
+        do_D_v(LAST - 3, 0, 4)
+        do_C_pe(LAST - 1, 0, 4)
+        do_M(4 * LAST + 2)
+        do_M(4 * LAST + 3)
+        do_V(4 * LAST)
+        do_S(4 * LAST + 1)
+        do_V(4 * LAST + 1)
+        do_C_s(LAST - 1, 0, 4)
+        do_S(4 * LAST + 2)
+        do_S(4 * LAST + 3)
+        do_C_h(LAST - 1, 0, 4, True)
+        do_QA(LAST, 0, 2)
         do_C_m(LAST - 1, 0, 4)
+        do_D_pe(LAST - 2, 0, 4)
         do_D_s(LAST - 2, 0, 4)
         do_D_v(LAST - 2, 0, 4)
-        do_C_h(LAST, 0, 2)
-        do_C_m(LAST, 0, 2)
+        do_C_pe(LAST, 0, 2)
+        do_V(4 * LAST + 2)
+        do_V(4 * LAST + 3)
+        do_C_h(LAST, 0, 2, True)
         do_C_s(LAST, 0, 2)
         do_D_pe(LAST - 1, 0, 4)
+        do_QA(LAST, 2, 2)
         do_C_pe(LAST, 2, 2)
+        do_C_m(LAST, 0, 2)
         do_D_s(LAST - 1, 0, 4)
+        do_C_h(LAST, 2, 2, True)
         do_D_v(LAST - 1, 0, 4)
-        do_C_h(LAST, 2, 2)
-        do_C_m(LAST, 2, 2)
         do_C_s(LAST, 2, 2)
         do_D_pe(LAST, 0, 2)
+        do_C_m(LAST, 2, 2)
         do_D_s(LAST, 0, 2)
-        do_D_pe(LAST, 2, 2)
         do_D_v(LAST, 0, 2)
+        do_D_pe(LAST, 2, 2)
         do_D_s(LAST, 2, 2)
         do_D_v(LAST, 2, 2)

@@ -18,7 +18,7 @@ FLOPS = 2 * B * D * F + 2 * B * D * C + 2 * D * C * C + 3 * B * C * C
 PREFETCH = 5
 N_MACRO = B // (4 * P)
 LAST = N_MACRO - 1
-E_SPLIT = 80
+E_SPLIT = 64
 
 
 def tile_minerva_detex_pb_t_kernel(tc, f_n, ex_n, ex_classes, class_reps, out):
@@ -419,12 +419,13 @@ def tile_minerva_detex_pb_t_kernel(tc, f_n, ex_n, ex_classes, class_reps, out):
             if m == 1:
                 tables_3()
             do_E(4 * c + 1, True, 0, E_SPLIT)
+            if m == 1:
+                tables_4()
             do_E(4 * c, True)
             do_V(4 * b + 1)
             do_E(4 * c + 2, False)
             do_E(4 * c + 3, False)
             if m == 1:
-                tables_4()
                 tables_5()
             do_Q(2 * c)
             do_M(4 * b + 2)

from contextlib import ExitStack

import concourse.mybir as mybir
from concourse.masks import make_identity

F32 = mybir.dt.float32
BF16 = mybir.dt.bfloat16
U32 = mybir.dt.uint32
U8 = mybir.dt.uint8
FP8X4 = mybir.dt.float8_e4m3fn_x4
ACT = mybir.ActivationFunctionType
ALU = mybir.AluOpType

P = 128
B, D, F, C = 8192, 512, 1024, 128
FLOPS = 2 * B * D * F + 2 * B * D * C + 2 * D * C * C + 3 * B * C * C

PREFETCH = 5
N_MACRO = B // (4 * P)
LAST = N_MACRO - 1
E_SPLIT = 64


def tile_minerva_detex_pb_t_kernel(tc, f_n, ex_n, ex_classes, class_reps, out):
    nc = tc.nc
    with ExitStack() as ctx:
        const = ctx.enter_context(tc.tile_pool(name="const", bufs=1))
        fpool = ctx.enter_context(tc.tile_pool(name="fpool", bufs=2 * (PREFETCH + 2)))
        fgp = ctx.enter_context(tc.tile_pool(name="fgp", bufs=4))
        fcp = ctx.enter_context(tc.tile_pool(name="fcp", bufs=5))
        s2p = ctx.enter_context(tc.tile_pool(name="s2p", bufs=4))
        agp = ctx.enter_context(tc.tile_pool(name="agp", bufs=3))
        acp = ctx.enter_context(tc.tile_pool(name="acp", bufs=3))
        e3p = ctx.enter_context(tc.tile_pool(name="e3p", bufs=4))
        ps_x = ctx.enter_context(tc.psum_pool(name="ps_x", bufs=4))
        ps_m = ctx.enter_context(tc.psum_pool(name="ps_m", bufs=3))
        ps_e = ctx.enter_context(tc.psum_pool(name="ps_e", bufs=1))
        ctx.enter_context(tc.manual_schedule())

        def bank(pool, shape, dtype=F32):
            return pool.tile(shape, dtype, name="bank", tag="bank")

        f_sbs = []

        def load_f(h):
            f_sb = fpool.tile([P, 2 * F], BF16, name="f_sb", tag="f_sb")
            nc.sync.dma_start(
                out=f_sb[:].rearrange("p (i k) -> p i k", i=2),
                in_=f_n[256 * h : 256 * (h + 1), :].rearrange("(p i) k -> p i k", i=2),
            )
            f_sbs.append(f_sb)

        f_0 = fpool.tile([P, 2 * F], BF16, name="f_sb", tag="f_sb")
        f_sbs.append(f_0)

        def load_f0(i):
            nc.sync.dma_start(
                out=f_0[:, i * F : (i + 1) * F], in_=f_n[0:256, :].rearrange("(p i) k -> p i k", i=2)[:, i, :]
            )

        load_f0(0)
        ex_rows = ex_n.rearrange("(p t) k -> p t k", t=4)
        ex_sbs = []
        for t in range(4):
            ex_sb = const.tile([P, F], BF16, name="ex_sb%d" % t)
            nc.sync.dma_start(out=ex_sb[:], in_=ex_rows[:, t, :])
            ex_sbs.append(ex_sb)
        load_f0(1)
        load_f(1)
        load_f(2)
        load_f(3)
        exc_sb = const.tile([P, 4 * C], BF16, name="exc_sb")
        nc.sync.dma_start(
            out=exc_sb[:].rearrange("p (t j) -> p t j", t=4),
            in_=ex_classes.rearrange("(p t) j -> p t j", t=4),
        )
        r_sb = const.tile([P, C], BF16, name="r_sb")
        nc.sync.dma_start(out=r_sb[:], in_=class_reps)
        for h in range(4, 2 * PREFETCH + 2):
            load_f(h)

        ident = const.tile([P, P], F32, name="ident")
        make_identity(nc, ident[:])
        ident_b = const.tile([P, P], BF16, name="ident_b")
        make_identity(nc, ident_b[:])
        warm = const.tile([P, 1], F32, name="warm")
        nc.vector.memset(warm[:], 1.0)
        nc.scalar.activation(out=warm[:], in_=warm[:], func=ACT.Sqrt)
        quarter = const.tile([P, P], F32, name="quarter")
        nc.gpsimd.memset(quarter[:], 0.25)
        sel = const.tile([P, P], BF16, name="sel")
        nc.gpsimd.memset(sel[:], 1.0 / 32.0)
        nc.gpsimd.memset(sel[96:128, :], 0.0)

        xts = {}
        fgs = {}
        fcs = {}
        sts = {}
        s2s = {}
        ags = {}
        acs = {}
        c3 = {}

        def transposes(xt, words):
            for g in range(2):
                for u in range(2):
                    c0 = 256 * g + 128 * u
                    nc.tensor.transpose(xt[:, g, u, :], words[:, c0 : c0 + P], ident[:])

        def copy_out(words, xt, on_vector, b0=0, b1=P):
            dst = words.bitcast(F32).rearrange("p (g b u) -> p g b u", g=2, u=2)[:, :, b0:b1, :]
            src = xt[:].rearrange("p g u b -> p g b u")[:, :, b0:b1, :]
            if on_vector:
                nc.vector.tensor_copy(out=dst, in_=src)
            else:
                nc.scalar.copy(out=dst, in_=src)

        def do_T(i):
            h, half = divmod(i, 2)
            xt = bank(ps_x, [P, 2, 2, P])
            transposes(xt, f_sbs[h][:].bitcast(F32)[:, 512 * half : 512 * (half + 1)])
            xts[i] = xt

        def do_E(i, on_vector, b0=0, b1=P):
            h, half = divmod(i, 2)
            if h not in fgs:
                fgs[h] = fgp.tile([P, 2048], BF16, name="fg", tag="fg", align_bytes=64)
            copy_out(fgs[h][:, 1024 * half : 1024 * (half + 1)], xts[i], on_vector, b0, b1)

        def do_Q(h):
            fc = fcp.tile([P, 512], U32, name="fc", tag="fc", align_bytes=64)
            fs = fcp.tile([P, 512], U8, name="fs", tag="fs", align_bytes=64)
            nc.vector.quantize_mx(out=fc[:].bitcast(FP8X4), scales=fs[:], in_=fgs[h][:])
            fcs[h] = (fc, fs)

        def do_Q0(half):
            if half == 0:
                fc = fcp.tile([P, 512], U32, name="fc", tag="fc", align_bytes=64)
                fs = fcp.tile([P, 512], U8, name="fs", tag="fs", align_bytes=64)
                fcs[0] = (fc, fs)
            fc, fs = fcs[0]
            cols = slice(256 * half, 256 * (half + 1))
            nc.vector.quantize_mx(
                out=fc[:, cols].bitcast(FP8X4), scales=fs[:, cols], in_=fgs[0][:, 1024 * half : 1024 * (half + 1)]
            )

        ex_banks = []
        ex_gs = []
        ex_cs = []

        def ex_T(t):
            xe = bank(ps_m if t < 3 else ps_e, [P, 2, 2, P])
            transposes(xe, ex_sbs[t][:].bitcast(F32))
            ex_banks.append(xe)

        def ex_E(t, on_vector):
            exg = const.tile([P, 1024], BF16, name="exg%d" % t, align_bytes=64)
            copy_out(exg[:], ex_banks[t], on_vector)
            ex_gs.append(exg)

        def ex_Q(t):
            ex_c = const.tile([P, 256], U32, name="ex_c%d" % t, align_bytes=64)
            ex_s = const.tile([P, 256], U8, name="ex_s%d" % t, align_bytes=64)
            nc.vector.quantize_mx(out=ex_c[:].bitcast(FP8X4), scales=ex_s[:], in_=ex_gs[t][:])
            ex_cs.append((ex_c, ex_s))

        def do_M(i):
            h, half = divmod(i, 2)
            fc, fs = fcs[h]
            st = bank(ps_m, [P, 4, P])
            for t in range(4):
                ex_c, ex_s = ex_cs[t]
                for g in range(2):
                    r0 = (2 * half + g) * P
                    nc.tensor.matmul_mx(
                        out=st[:, t, :],
                        lhsT=ex_c[:, g * P : (g + 1) * P].bitcast(FP8X4),
                        lhsT_scale=ex_s[:, g * P : (g + 1) * P],
                        rhs=fc[:, r0 : r0 + P].bitcast(FP8X4),
                        rhs_scale=fs[:, r0 : r0 + P],
                        start=(g == 0),
                        stop=(g == 1),
                    )
            sts[i] = st

        def do_S(i):
            s2 = s2p.tile([P, 512], F32, name="s2", tag="s2")
            nc.scalar.activation(out=s2[:].rearrange("p (t b) -> p t b", t=4), in_=sts[i][:], func=ACT.Square)
            s2s[i] = s2

        def do_V(i):
            m, j = divmod(i, 4)
            if j == 0:
                ags[m] = agp.tile([P, 2048], BF16, name="ag", tag="ag", align_bytes=64)
            nc.vector.tensor_tensor(
                out=ags[m][:, 512 * j : 512 * (j + 1)].rearrange("p (c i t) -> p c t i", i=4, t=4),
                in0=sts[i][:].rearrange("p t (c i) -> p c t i", i=4),
                in1=s2s[i][:].rearrange("p (t c i) -> p c t i", t=4, i=4),
                op=ALU.mult,
            )

        def do_QA(m, j0, nj):
            ac = acp.tile([P, nj * P], U32, name="ac", tag="ac%d" % j0, align_bytes=64)
            asc = acp.tile([P, nj * P], U8, name="asc", tag="asc%d" % j0, align_bytes=64)
            nc.vector.quantize_mx(
                out=ac[:].bitcast(FP8X4), scales=asc[:], in_=ags[m][:, 512 * j0 : 512 * (j0 + nj)]
            )
            acs[(m, j0)] = (ac, asc)

        excT = const.tile([P, 4, P], BF16, name="excT")
        ecg = const.tile([P, 512], BF16, name="ecg", align_bytes=64)
        ecr_c = const.tile([P, P], U32, name="ecr_c", align_bytes=64)
        ecr_s = const.tile([P, P], U8, name="ecr_s", align_bytes=64)
        rTm2 = const.tile([P, P], BF16, name="rTm2")
        r2T = const.tile([P, P], F32, name="r2T")
        rr_w = const.tile([P, P], BF16, name="rr_w")
        t_bank = []
        ec_bank = []

        def tables_1():
            xc_ps = bank(ps_x, [P, 4, P], BF16)
            for t in range(4):
                nc.tensor.transpose(xc_ps[:, t, :], exc_sb[:, t * P : (t + 1) * P], ident_b[:])
            rt_ps = bank(ps_x, [P, P], BF16)
            nc.tensor.transpose(rt_ps[:], r_sb[:], ident_b[:])
            t_bank.extend([xc_ps, rt_ps])

        def tables_1v():
            xc_ps, rt_ps = t_bank
            nc.scalar.copy(out=excT[:], in_=xc_ps[:])
            nc.vector.tensor_scalar(out=rTm2[:], in0=rt_ps[:], scalar1=-2.0, scalar2=None, op0=ALU.mult)
            nc.gpsimd.tensor_tensor(out=r2T[:], in0=rTm2[:], in1=rTm2[:], op=ALU.mult)

        def tables_2():
            ec_ps = bank(ps_e, [P, 4, P])
            for t in range(4):
                nc.tensor.matmul(out=ec_ps[:, t, :], lhsT=excT[:, t, :], rhs=r_sb[:], start=True, stop=True)
            rr_ps = bank(ps_x, [P, P])
            nc.tensor.matmul(out=rr_ps[:], lhsT=quarter[:], rhs=r2T[:], start=True, stop=True)
            ec_bank.extend([ec_ps, rr_ps])

        def tables_3():
            nc.vector.tensor_copy(
                out=ecg[:].rearrange("p (c t) -> p c t", t=4), in_=ec_bank[0][:].rearrange("p t c -> p c t")
            )

        def tables_4():
            nc.vector.quantize_mx(out=ecr_c[:].bitcast(FP8X4), scales=ecr_s[:], in_=ecg[:])

        def tables_5():
            rr_ps = ec_bank[1]
            rrf = const.tile([P, P], F32, name="rrf")
            nc.scalar.copy(out=rrf[:], in_=rr_ps[:])
            rr_h = const.tile([P, P], BF16, name="rr_h")
            nc.gpsimd.tensor_copy(out=rr_h[:], in_=rrf[:])
            rr_d = const.tile([P, P], F32, name="rr_d")
            nc.gpsimd.tensor_tensor(out=rr_d[:], in0=rrf[:], in1=rr_h[:], op=ALU.subtract)
            rr_m = const.tile([P, P], BF16, name="rr_m")
            nc.gpsimd.tensor_copy(out=rr_m[:], in_=rr_d[:])
            nc.gpsimd.memset(rr_w[:], 0.0)
            nc.gpsimd.tensor_copy(out=rr_w[0:32, :], in_=rr_h[0:32, :])
            nc.gpsimd.tensor_copy(out=rr_w[32:64, :], in_=rr_m[32:64, :])
            nc.gpsimd.tensor_tensor(
                out=rr_w[64:96, :], in0=rr_d[64:96, :], in1=rr_m[64:96, :], op=ALU.subtract
            )

        def do_C_pe(m, j0, nj):
            ac, asc = acs[(m, j0)]
            eT = bank(ps_e if nj == 4 else ps_x, [P, nj * P])
            nc.tensor.matmul_mx(
                out=eT[:],
                lhsT=ecr_c[:].bitcast(FP8X4),
                lhsT_scale=ecr_s[:],
                rhs=ac[:].bitcast(FP8X4),
                rhs_scale=asc[:],
                start=True,
                stop=True,
            )
            eb = bank(ps_x, [P, nj, P])
            for j in range(nj):
                jc = slice(j * P, (j + 1) * P)
                nc.tensor.matmul_mx(
                    out=eb[:, j, :],
                    lhsT=ac[:, jc].bitcast(FP8X4),
                    lhsT_scale=asc[:, jc],
                    rhs=ecr_c[:].bitcast(FP8X4),
                    rhs_scale=ecr_s[:],
                    start=True,
                    stop=True,
                )
            c3[(m, j0)] = {"eT": eT, "eb": eb}

        def do_C_h(m, j0, nj, on_vector=False):
            t = c3[(m, j0)]
            t["eh"] = e3p.tile([P, nj * P], BF16, name="eh", tag="eh")
            t["em"] = e3p.tile([P, nj * P], BF16, name="em", tag="em")
            if on_vector:
                nc.vector.tensor_copy(out=t["eh"][:], in_=t["eT"][:])
            else:
                nc.scalar.copy(out=t["eh"][:], in_=t["eT"][:])

        def do_C_m(m, j0, nj):
            t = c3[(m, j0)]
            nc.vector.tensor_tensor(out=t["em"][:], in0=t["eT"][:], in1=t["eh"][:], op=ALU.subtract)

        def do_C_s(m, j0, nj):
            ee = e3p.tile([P, nj], F32, name="ee", tag="ee")
            for j in range(nj):
                junk = e3p.tile([P, P], BF16, name="junk", tag="junk")
                nc.scalar.activation(
                    out=junk[:], in_=c3[(m, j0)]["eb"][:, j, :], func=ACT.Square, accum_out=ee[:, j : j + 1]
                )
            c3[(m, j0)]["ee"] = ee

        def do_D_pe(m, j0, nj):
            db = bank(ps_x, [P, nj, P])
            eh, em = c3[(m, j0)]["eh"], c3[(m, j0)]["em"]
            for j in range(nj):
                jc = slice(j * P, (j + 1) * P)
                nc.tensor.matmul(out=db[:, j, :], lhsT=sel[:], rhs=rr_w[:], start=True, stop=False)
                nc.tensor.matmul(out=db[:, j, :], lhsT=em[:, jc], rhs=rTm2[:], start=False, stop=False)
                nc.tensor.matmul(out=db[:, j, :], lhsT=eh[:, jc], rhs=rTm2[:], start=False, stop=True)
            c3[(m, j0)]["db"] = db

        def do_D_s(m, j0, nj):
            sq = e3p.tile([P, nj * P], F32, name="sq", tag="sq")
            for j in range(nj):
                nc.scalar.activation(
                    out=sq[:, j * P : (j + 1) * P],
                    in_=c3[(m, j0)]["db"][:, j, :],
                    func=ACT.Sqrt,
                    bias=c3[(m, j0)]["ee"][:, j : j + 1],
                    scale=1.0,
                )
            c3[(m, j0)]["sq"] = sq

        def do_D_v(m, j0, nj):
            o = e3p.tile([P, nj * P], F32, name="o", tag="o")
            eng = nc.vector if m >= LAST - 1 else nc.gpsimd
            eng.tensor_scalar(
                out=o[:], in0=c3[(m, j0)]["sq"][:], scalar1=-1.0, scalar2=0.0, op0=ALU.mult, op1=ALU.add
            )
            r0 = 512 * m + P * j0
            nc.sync.dma_start(
                out=out[r0 : r0 + nj * P, :].rearrange("(q p i) k -> p q i k", p=P, i=2),
                in_=o[:].rearrange("p (q i k) -> p q i k", i=2, k=C),
            )

        do_T(0)
        do_E(0, False)
        for t in range(4):
            ex_T(t)
        ex_E(0, True)
        ex_E(1, False)
        do_Q0(0)
        ex_Q(0)
        ex_E(2, True)
        ex_E(3, False)
        ex_Q(1)
        do_T(1)
        ex_Q(2)
        ex_Q(3)
        do_M(0)
        do_E(1, True)
        do_T(2)
        do_T(3)
        do_S(0)
        do_Q0(1)
        do_E(2, False)
        do_E(3, True)
        do_M(1)
        do_T(4)
        do_T(5)
        do_Q(1)
        do_S(1)
        do_V(0)
        do_E(4, False)
        do_E(5, True)
        do_M(2)
        do_M(3)
        do_V(1)
        do_Q(2)
        do_T(6)
        do_T(7)
        do_S(2)
        do_E(6, False)
        do_S(3)
        do_E(7, False)
        do_M(4)
        do_M(5)
        do_V(2)
        do_V(3)
        tables_1()
        do_QA(0, 0, 4)
        do_Q(3)
        tables_1v()
        do_S(4)

        def ok(m):
            return 0 <= m < N_MACRO

        for m in range(1, LAST):
            y, z, a, b, c = m - 3, m - 2, m - 1, m, m + 1
            if ok(m + PREFETCH):
                load_f(2 * (m + PREFETCH))
                load_f(2 * (m + PREFETCH) + 1)
            for j in (1, 0, 2, 3):
                do_T(4 * c + j)
            if m == 1:
                tables_2()
            if ok(z):
                do_C_m(z, 0, 4)
            if ok(y):
                do_D_s(y, 0, 4)
                do_D_v(y, 0, 4)
            do_V(4 * b)
            do_E(4 * c + 1, False, E_SPLIT, P)
            do_S(4 * b + 1)
            if m == 1:
                tables_3()
            do_E(4 * c + 1, True, 0, E_SPLIT)
            if m == 1:
                tables_4()
            do_E(4 * c, True)
            do_V(4 * b + 1)
            do_E(4 * c + 2, False)
            do_E(4 * c + 3, False)
            if m == 1:
                tables_5()
            do_Q(2 * c)
            do_M(4 * b + 2)
            do_M(4 * b + 3)
            do_S(4 * b + 2)
            do_S(4 * b + 3)
            do_V(4 * b + 2)
            do_V(4 * b + 3)
            do_C_pe(a, 0, 4)
            if ok(z):
                do_D_pe(z, 0, 4)
            do_Q(2 * c + 1)
            do_QA(b, 0, 4)
            do_M(4 * c)
            do_M(4 * c + 1)
            do_C_s(a, 0, 4)
            do_C_h(a, 0, 4)
            do_S(4 * c)

        do_C_m(LAST - 2, 0, 4)
        do_D_s(LAST - 3, 0, 4)
        do_D_v(LAST - 3, 0, 4)
        do_C_pe(LAST - 1, 0, 4)
        do_M(4 * LAST + 2)
        do_M(4 * LAST + 3)
        do_V(4 * LAST)
        do_S(4 * LAST + 1)
        do_V(4 * LAST + 1)
        do_C_s(LAST - 1, 0, 4)
        do_S(4 * LAST + 2)
        do_S(4 * LAST + 3)
        do_C_h(LAST - 1, 0, 4, True)
        do_QA(LAST, 0, 2)
        do_C_m(LAST - 1, 0, 4)
        do_D_pe(LAST - 2, 0, 4)
        do_D_s(LAST - 2, 0, 4)
        do_D_v(LAST - 2, 0, 4)
        do_C_pe(LAST, 0, 2)
        do_V(4 * LAST + 2)
        do_V(4 * LAST + 3)
        do_C_h(LAST, 0, 2, True)
        do_C_s(LAST, 0, 2)
        do_D_pe(LAST - 1, 0, 4)
        do_QA(LAST, 2, 2)
        do_C_pe(LAST, 2, 2)
        do_C_m(LAST, 0, 2)
        do_D_s(LAST - 1, 0, 4)
        do_C_h(LAST, 2, 2, True)
        do_D_v(LAST - 1, 0, 4)
        do_C_s(LAST, 2, 2)
        do_D_pe(LAST, 0, 2)
        do_C_m(LAST, 2, 2)
        do_D_s(LAST, 0, 2)
        do_D_v(LAST, 0, 2)
        do_D_pe(LAST, 2, 2)
        do_D_s(LAST, 2, 2)
        do_D_v(LAST, 2, 2)
